import numpy as np
import ml_dtypes


def mxq(x, axis, fmt="e4m3"):
    dtype, down = {"e4m3": (ml_dtypes.float8_e4m3fn, 7), "e5m2": (ml_dtypes.float8_e5m2, 14)}[fmt]
    v = np.moveaxis(np.asarray(x, np.float32).astype(ml_dtypes.bfloat16).astype(np.float64), axis, -1)
    blocks = v.reshape(v.shape[:-1] + (-1, 32))
    amax = np.abs(blocks).max(-1, keepdims=True)
    byte = np.maximum(np.where(amax > 0, np.frexp(amax)[1] - 1 + 127, 0) - down, 1)
    scale = np.exp2(byte - 127.0)
    codes = (blocks / scale).astype(np.float32).astype(dtype).astype(np.float64)
    return np.moveaxis((codes * scale).reshape(v.shape), -1, axis)


WIDE = False


def mx_kscale(k):
    if not WIDE:
        return np.ones(k)
    levels = np.array([20, -20, 10, -10, 0])
    a = np.random.permutation(np.resize(levels, k // 512 * 4)).reshape(k // 512, 4)
    idx = np.arange(k)
    return np.exp2(a[idx // 512, idx % 128 // 32])


BF16 = ml_dtypes.bfloat16


def bf(x):
    return np.asarray(x, np.float32).astype(BF16)


def f64(x):
    return np.asarray(x).astype(np.float64)


B, C, D = 1024, 2048, 1024
GS = 256.0


def sigmoid(v):
    return 1.0 / (1.0 + np.exp(-v))


def setup_inputs():
    s = mx_kscale(B)
    r = np.sqrt(s.max() / s)[:, None]
    a = 1.0 / np.sqrt(D)
    x0 = bf((np.random.standard_normal((B, D)) + np.random.uniform(-1.0, 1.0, (B, 1))) * a)
    mean = bf(np.random.uniform(0.0, 1.0, (C, D)) * np.random.uniform(0.5, 1.5, (C, 1)) * a)
    rho = bf(np.random.uniform(0.0, 1.0, (C, D)))
    g = np.random.standard_normal((B, C)) * np.exp2(np.random.randint(-12, 1, (B, 1))) * GS
    xf, mf = f64(x0), f64(mean)
    sigma = np.log1p(np.exp(f64(rho)))
    w = 1.0 / (2.0 * sigma * sigma)
    quad = (xf * xf) @ w.T - 2.0 * (xf @ (mf * w).T) + np.sum(mf * mf * w, axis=-1)
    return {"x": bf(xf * r), "mean": mean, "rho": rho, "quad": np.asarray(quad, np.float32), "grad_out": bf(g / (r * r))}


def reference(x, mean, rho, quad, grad_out):
    x, mean, rho = f64(x), f64(mean), f64(rho)
    e = f64(grad_out) * np.exp(-f64(quad))
    eq = mxq(e, 0, "e5m2")
    p2 = eq.T @ mxq(x * x, 0, "e4m3")
    p1 = eq.T @ mxq(x, 0, "e4m3")
    s0 = np.sum(e, axis=0)[:, None]
    sigma = np.log1p(np.exp(rho))
    return (p2 - 2.0 * mean * p1 + mean * mean * s0) * sigmoid(rho) / (sigma * sigma * sigma)

@@ -1,0 +1,362 @@
+from contextlib import ExitStack
+
+import concourse.mybir as mybir
+
+F32 = mybir.dt.float32
+BF16 = mybir.dt.bfloat16
+U32 = mybir.dt.uint32
+U8 = mybir.dt.uint8
+E4M3_X4 = mybir.dt.float8_e4m3fn_x4
+E5M2_X4 = mybir.dt.float8_e5m2_x4
+ACT = mybir.ActivationFunctionType
+ALU = mybir.AluOpType
+
+BATCH, CLASSES, FEATURES = 1024, 2048, 1024
+P = 128
+PACK = 4
+K_PASS = P * PACK
+PASSES = BATCH // K_PASS
+WIDTH = 512
+CHUNKS = CLASSES // WIDTH
+CHUNK_TILES = WIDTH // P
+FEATURE_HALVES = FEATURES // WIDTH
+RUN = 4
+ROUND_TILES = 2 * CHUNK_TILES
+LEAD_PAIRS = 1
+
+FLOPS = 2 * 2 * BATCH * CLASSES * FEATURES
+
+
+def tile_dynamic_estimator_v_kernel(tc, x, mean, rho, quad, grad_out, out):
+    nc = tc.nc
+    with ExitStack() as stack:
+
+        def sbuf_pool(name, bufs):
+            return stack.enter_context(tc.tile_pool(name=name, bufs=bufs))
+
+        def psum_pool(name, bufs):
+            return stack.enter_context(tc.psum_pool(name=name, bufs=bufs))
+
+        keep = sbuf_pool("keep", 1)
+        quad_pool = sbuf_pool("quad", 2 * PASSES)
+        rows_pool = sbuf_pool("rows", 6)
+        grouped_pool = sbuf_pool("grouped", 4)
+        codes_pool = sbuf_pool("codes", 2)
+        rho_pool = sbuf_pool("rho", 2)
+        mean_pool = sbuf_pool("mean", 2)
+        tanh_pool = sbuf_pool("tanh", ROUND_TILES)
+        chain_pool = sbuf_pool("chain", ROUND_TILES)
+        acc_pool = sbuf_pool("acc", ROUND_TILES)
+        sums_pool = sbuf_pool("sums", 2)
+        p1_pool = psum_pool("p1", 3)
+        p2_pool = psum_pool("p2", 4)
+        s0_pool = psum_pool("s0", 1)
+
+        stack.enter_context(tc.manual_schedule())
+
+        x_codes = keep.tile([P, PASSES, FEATURES], U32, align_bytes=64)
+        x_scales = keep.tile([P, PASSES, FEATURES], U8, align_bytes=64)
+        xx_codes = keep.tile([P, PASSES, FEATURES], U32, align_bytes=64)
+        xx_scales = keep.tile([P, PASSES, FEATURES], U8, align_bytes=64)
+        half_column = keep.tile([P, 1], F32)
+        nc.vector.memset(half_column[:], 0.5)
+
+        x_rows, e_rows, grad_rows, e_grouped = {}, {}, {}, {}
+        e_codes, e_scales, half_s0, s0_bank = {}, {}, {}, {}
+        rho_rows, mean_rows, tanh_half, chain, acc = {}, {}, {}, {}, {}
+        p1, p2 = {}, {}
+
+        def piece(index):
+            return slice(index * WIDTH, (index + 1) * WIDTH)
+
+        def batch_rows(source, c, cols):
+            rows = slice(c * K_PASS, (c + 1) * K_PASS)
+            return source[rows, cols].rearrange("(p j) w -> p j w", j=PACK)
+
+        def flat(grouped):
+            return grouped[:].rearrange("p w j -> p (w j)")
+
+        def load_bf16_rows(source, c, cols):
+            rows = rows_pool.tile([P, PACK, WIDTH], BF16)
+            nc.sync.dma_start(out=rows[:], in_=batch_rows(source, c, cols))
+            return rows
+
+        def load_x(c, h):
+            x_rows[c, h] = load_bf16_rows(x, c, piece(h))
+
+        def load_e(k, c):
+            quad_rows = quad_pool.tile([P, PACK, WIDTH], F32)
+            nc.sync.dma_start(out=quad_rows[:], in_=batch_rows(quad, c, piece(k)))
+            e_rows[k, c] = quad_rows
+            grad_rows[k, c] = load_bf16_rows(grad_out, c, piece(k))
+
+        def load_class_rows(pool, source, k):
+            class_rows = pool.tile([P, CHUNK_TILES, FEATURES], BF16)
+            nc.sync.dma_start(
+                out=class_rows[:], in_=source[piece(k), :].rearrange("(t p) d -> p t d", p=P)
+            )
+            return class_rows
+
+        def regroup(copy, grouped, rows, cols):
+            copy(
+                out=grouped[:, cols, :].rearrange("p (w i) j -> p w j i", i=RUN),
+                in_=rows[:, :, cols].rearrange("p j (w i) -> p w j i", i=RUN),
+            )
+
+        def grouped_tile():
+            grouped = grouped_pool.tile([P, WIDTH, PACK], BF16, align_bytes=64)
+            return grouped
+
+        def quantise_x(c, h):
+            x_grouped = grouped_tile()
+            squared = grouped_tile()
+            halves = (slice(0, WIDTH // 2), slice(WIDTH // 2, WIDTH))
+            for cols in halves:
+                regroup(nc.vector.tensor_copy, x_grouped, x_rows[c, h], cols)
+            for cols in halves:
+                nc.vector.tensor_tensor(
+                    out=squared[:, cols, :],
+                    in0=x_grouped[:, cols, :],
+                    in1=x_grouped[:, cols, :],
+                    op=ALU.mult,
+                )
+            nc.vector.quantize_mx(
+                out=x_codes[:, c, piece(h)].bitcast(E4M3_X4),
+                scales=x_scales[:, c, piece(h)],
+                in_=flat(x_grouped),
+            )
+            nc.vector.quantize_mx(
+                out=xx_codes[:, c, piece(h)].bitcast(E4M3_X4),
+                scales=xx_scales[:, c, piece(h)],
+                in_=flat(squared),
+            )
+
+        def exponential(k, c):
+            nc.scalar.activation(out=e_rows[k, c][:], in_=e_rows[k, c][:], func=ACT.Exp, scale=-1.0)
+
+        def multiply(k, c):
+            nc.vector.tensor_tensor(
+                out=e_rows[k, c][:], in0=e_rows[k, c][:], in1=grad_rows[k, c][:], op=ALU.mult
+            )
+
+        def regroup_e(k, c):
+            e_grouped[k, c] = grouped_tile()
+            regroup(nc.scalar.copy, e_grouped[k, c], e_rows[k, c], slice(0, WIDTH))
+
+        def quantise_e(k, c):
+            if c == 0:
+                codes = codes_pool.tile([P, PASSES, WIDTH], U32, align_bytes=64)
+                scales = codes_pool.tile([P, PASSES, WIDTH], U8, align_bytes=64)
+                e_codes[k], e_scales[k] = codes, scales
+            nc.vector.quantize_mx(
+                out=e_codes[k][:, c, :].bitcast(E5M2_X4),
+                scales=e_scales[k][:, c, :],
+                in_=flat(e_grouped[k, c]),
+            )
+
+        def column_sums(k):
+            bank = s0_pool.tile([P, CHUNK_TILES], F32)
+            slices = [(c, j) for c in range(PASSES) for j in range(PACK)]
+            for t in range(CHUNK_TILES):
+                for c, j in slices:
+                    nc.tensor.matmul(
+                        out=bank[:, t : t + 1],
+                        lhsT=e_rows[k, c][:, j, t * P : (t + 1) * P],
+                        rhs=half_column[:],
+                        start=((c, j) == slices[0]),
+                        stop=((c, j) == slices[-1]),
+                    )
+            s0_bank[k] = bank
+
+        def copy_sums(k):
+            sums = sums_pool.tile([P, CHUNK_TILES], F32)
+            nc.vector.tensor_copy(out=sums[:], in_=s0_bank[k][:])
+            half_s0[k] = sums
+
+        def tanh_rho(i):
+            k, t = divmod(i, CHUNK_TILES)
+            tanh_tile = tanh_pool.tile([P, FEATURES], F32)
+            nc.scalar.activation(
+                out=tanh_tile[:], in_=rho_rows[k][:, t, :], func=ACT.Tanh, scale=0.5
+            )
+            tanh_half[i] = tanh_tile
+
+        def logarithms(pair):
+            for i in pair:
+                chain_tile = chain_pool.tile([P, FEATURES], F32)
+                nc.scalar.activation(
+                    out=chain_tile[:],
+                    in_=tanh_half[i][:],
+                    func=ACT.Ln,
+                    scale=-0.5,
+                    bias=half_column[:],
+                )
+                chain[i] = chain_tile
+            for i in pair:
+                nc.scalar.activation(out=chain[i][:], in_=chain[i][:], func=ACT.Ln, scale=-1.0)
+
+        def inverse_cubes(pair):
+            for i in pair:
+                nc.scalar.activation(out=chain[i][:], in_=chain[i][:], func=ACT.Exp, scale=-3.0)
+
+        def product(bank, i, codes, scales, h):
+            k, t = divmod(i, CHUNK_TILES)
+            classes = slice(t * P, (t + 1) * P)
+            for c in range(PASSES):
+                nc.tensor.matmul_mx(
+                    out=bank[:],
+                    lhsT=e_codes[k][:, c, classes].bitcast(E5M2_X4),
+                    lhsT_scale=e_scales[k][:, c, classes],
+                    rhs=codes[:, c, piece(h)].bitcast(E4M3_X4),
+                    rhs_scale=scales[:, c, piece(h)],
+                    start=(c == 0),
+                    stop=(c == PASSES - 1),
+                )
+
+        def matmuls(pair):
+            for i in pair:
+                for h in range(FEATURE_HALVES):
+                    p1_bank = p1_pool.tile([P, WIDTH], F32)
+                    product(p1_bank, i, x_codes, x_scales, h)
+                    p1[i, h] = p1_bank
+            for i in pair:
+                for h in range(FEATURE_HALVES):
+                    p2_bank = p2_pool.tile([P, WIDTH], F32)
+                    product(p2_bank, i, xx_codes, xx_scales, h)
+                    p2[i, h] = p2_bank
+
+        def mean_tile(i):
+            k, t = divmod(i, CHUNK_TILES)
+            return mean_rows[k][:, t, :]
+
+        def mean_s0_minus_p1(i):
+            k, t = divmod(i, CHUNK_TILES)
+            acc_tile = acc_pool.tile([P, FEATURES], F32)
+            for h in range(FEATURE_HALVES):
+                nc.vector.scalar_tensor_tensor(
+                    out=acc_tile[:, piece(h)],
+                    in0=mean_tile(i)[:, piece(h)],
+                    scalar=half_s0[k][:, t : t + 1],
+                    in1=p1[i, h][:],
+                    op0=ALU.mult,
+                    op1=ALU.subtract,
+                )
+            acc[i] = acc_tile
+
+        def times_mean(i):
+            nc.vector.tensor_tensor(out=acc[i][:], in0=acc[i][:], in1=mean_tile(i), op=ALU.mult)
+
+        def plus_half_p2(i):
+            for h in range(FEATURE_HALVES):
+                nc.vector.scalar_tensor_tensor(
+                    out=acc[i][:, piece(h)],
+                    in0=p2[i, h][:],
+                    scalar=0.5,
+                    in1=acc[i][:, piece(h)],
+                    op0=ALU.mult,
+                    op1=ALU.add,
+                )
+
+        def times_one_plus_tanh(i):
+            nc.vector.scalar_tensor_tensor(
+                out=acc[i][:],
+                in0=tanh_half[i][:],
+                scalar=1.0,
+                in1=acc[i][:],
+                op0=ALU.add,
+                op1=ALU.mult,
+            )
+
+        def finish(i):
+            nc.vector.tensor_tensor(out=acc[i][:], in0=acc[i][:], in1=chain[i][:], op=ALU.mult)
+            nc.sync.dma_start(out=out[i * P : (i + 1) * P, :], in_=acc[i][:])
+
+        passes = range(PASSES)
+        for c in passes:
+            load_x(c, 0)
+            load_e(0, c)
+        for c in passes:
+            load_x(c, 1)
+        for c in passes:
+            load_e(1, c)
+        mean_rows[0] = load_class_rows(mean_pool, mean, 0)
+        rho_rows[0] = load_class_rows(rho_pool, rho, 0)
+        rho_rows[1] = load_class_rows(rho_pool, rho, 1)
+
+        for c in passes:
+            quantise_x(c, 0)
+            exponential(0, c)
+            multiply(0, c)
+        for c in passes:
+            regroup_e(0, c)
+        column_sums(0)
+        for c in passes:
+            quantise_e(0, c)
+            if c == PASSES - 1:
+                copy_sums(0)
+            quantise_x(c, 1)
+        matmuls((0, 1))
+        for c in passes:
+            exponential(1, c)
+        for i in range(ROUND_TILES):
+            tanh_rho(i)
+
+        for k in range(CHUNKS):
+            first = k * CHUNK_TILES
+            pair_a, pair_b = (first, first + 1), (first + 2, first + 3)
+            following = k + 1
+            more = following < CHUNKS
+            exp_turn = k % 2 == 1
+            round_start = (k // 2) * ROUND_TILES
+            round_tiles = list(range(round_start, round_start + ROUND_TILES))
+            round_pairs = [(i, i + 1) for i in round_tiles[::2]]
+            rho_step = inverse_cubes if exp_turn else logarithms
+
+            if k + 2 < CHUNKS:
+                for c in passes:
+                    load_e(k + 2, c)
+                rho_rows[k + 2] = load_class_rows(rho_pool, rho, k + 2)
+            if more:
+                mean_rows[following] = load_class_rows(mean_pool, mean, following)
+
+            if exp_turn and more:
+                for c in passes:
+                    exponential(following, c)
+            matmuls(pair_b)
+            for step in (mean_s0_minus_p1, times_mean, plus_half_p2, times_one_plus_tanh):
+                for i in pair_a:
+                    step(i)
+            if more:
+                for c in passes:
+                    multiply(following, c)
+            for pair in round_pairs[:LEAD_PAIRS]:
+                rho_step(pair)
+            if more:
+                for c in passes:
+                    regroup_e(following, c)
+                column_sums(following)
+            for pair in round_pairs[LEAD_PAIRS:]:
+                rho_step(pair)
+            if exp_turn and more:
+                for c in passes:
+                    exponential(following + 1, c)
+                for i in round_tiles:
+                    tanh_rho(i + ROUND_TILES)
+
+            for i in pair_b:
+                mean_s0_minus_p1(i)
+            if more:
+                quantise_e(following, 0)
+            for step in (times_mean, plus_half_p2):
+                for i in pair_b:
+                    step(i)
+            if more:
+                quantise_e(following, 1)
+                matmuls((first + CHUNK_TILES, first + CHUNK_TILES + 1))
+            times_one_plus_tanh(pair_b[0])
+            if more:
+                copy_sums(following)
+            times_one_plus_tanh(pair_b[1])
+            if exp_turn:
+                for i in round_tiles:
+                    finish(i)

@@ -58,8 +58,8 @@ def tile_dynamic_estimator_v_kernel(tc, x, mean, rho, quad, grad_out, out):
         x_scales = keep.tile([P, PASSES, FEATURES], U8, align_bytes=64)
         xx_codes = keep.tile([P, PASSES, FEATURES], U32, align_bytes=64)
         xx_scales = keep.tile([P, PASSES, FEATURES], U8, align_bytes=64)
-        half_column = keep.tile([P, 1], F32)
-        nc.vector.memset(half_column[:], 0.5)
+        halves = keep.tile([P, P], F32)
+        nc.vector.memset(halves[:], 0.5)
 
         x_rows, e_rows, grad_rows, e_grouped = {}, {}, {}, {}
         e_codes, e_scales, half_s0, s0_bank = {}, {}, {}, {}
@@ -110,10 +110,10 @@ def tile_dynamic_estimator_v_kernel(tc, x, mean, rho, quad, grad_out, out):
         def quantise_x(c, h):
             x_grouped = grouped_tile()
             squared = grouped_tile()
-            halves = (slice(0, WIDTH // 2), slice(WIDTH // 2, WIDTH))
-            for cols in halves:
+            parts = (slice(0, WIDTH // 2), slice(WIDTH // 2, WIDTH))
+            for cols in parts:
                 regroup(nc.vector.tensor_copy, x_grouped, x_rows[c, h], cols)
-            for cols in halves:
+            for cols in parts:
                 nc.vector.tensor_tensor(
                     out=squared[:, cols, :],
                     in0=x_grouped[:, cols, :],
@@ -154,24 +154,31 @@ def tile_dynamic_estimator_v_kernel(tc, x, mean, rho, quad, grad_out, out):
                 in_=flat(e_grouped[k, c]),
             )
 
-        def column_sums(k):
-            bank = s0_pool.tile([P, CHUNK_TILES], F32)
+        def pair_of_chunk(a):
+            return slice(2 * a, 2 * a + 2)
+
+        def column_sums(k, a):
+            if a == 0:
+                bank = s0_pool.tile([P, CHUNK_TILES, P], F32)
+                s0_bank[k] = bank
             slices = [(c, j) for c in range(PASSES) for j in range(PACK)]
-            for t in range(CHUNK_TILES):
+            for t in range(CHUNK_TILES)[pair_of_chunk(a)]:
                 for c, j in slices:
                     nc.tensor.matmul(
-                        out=bank[:, t : t + 1],
+                        out=s0_bank[k][:, t, :],
                         lhsT=e_rows[k, c][:, j, t * P : (t + 1) * P],
-                        rhs=half_column[:],
+                        rhs=halves[:],
                         start=((c, j) == slices[0]),
                         stop=((c, j) == slices[-1]),
                     )
-            s0_bank[k] = bank
 
-        def copy_sums(k):
-            sums = sums_pool.tile([P, CHUNK_TILES], F32)
-            nc.vector.tensor_copy(out=sums[:], in_=s0_bank[k][:])
-            half_s0[k] = sums
+        def copy_sums(k, a):
+            if a == 0:
+                sums = sums_pool.tile([P, CHUNK_TILES, 1], F32)
+                half_s0[k] = sums
+            nc.vector.tensor_copy(
+                out=half_s0[k][:, pair_of_chunk(a), :], in_=s0_bank[k][:, pair_of_chunk(a), 0:1]
+            )
 
         def tanh_rho(i):
             k, t = divmod(i, CHUNK_TILES)
@@ -189,7 +196,7 @@ def tile_dynamic_estimator_v_kernel(tc, x, mean, rho, quad, grad_out, out):
                     in_=tanh_half[i][:],
                     func=ACT.Ln,
                     scale=-0.5,
-                    bias=half_column[:],
+                    bias=halves[:, 0:1],
                 )
                 chain[i] = chain_tile
             for i in pair:
@@ -236,7 +243,7 @@ def tile_dynamic_estimator_v_kernel(tc, x, mean, rho, quad, grad_out, out):
                 nc.vector.scalar_tensor_tensor(
                     out=acc_tile[:, piece(h)],
                     in0=mean_tile(i)[:, piece(h)],
-                    scalar=half_s0[k][:, t : t + 1],
+                    scalar=half_s0[k][:, t, :],
                     in1=p1[i, h][:],
                     op0=ALU.mult,
                     op1=ALU.subtract,
@@ -289,11 +296,11 @@ def tile_dynamic_estimator_v_kernel(tc, x, mean, rho, quad, grad_out, out):
             multiply(0, c)
         for c in passes:
             regroup_e(0, c)
-        column_sums(0)
+        column_sums(0, 0)
         for c in passes:
             quantise_e(0, c)
             if c == PASSES - 1:
-                copy_sums(0)
+                copy_sums(0, 0)
             quantise_x(c, 1)
         matmuls((0, 1))
         for c in passes:
@@ -322,10 +329,14 @@ def tile_dynamic_estimator_v_kernel(tc, x, mean, rho, quad, grad_out, out):
             if exp_turn and more:
                 for c in passes:
                     exponential(following, c)
+            column_sums(k, 1)
             matmuls(pair_b)
-            for step in (mean_s0_minus_p1, times_mean, plus_half_p2, times_one_plus_tanh):
+            for step in (mean_s0_minus_p1, times_mean, plus_half_p2):
                 for i in pair_a:
                     step(i)
+            times_one_plus_tanh(pair_a[0])
+            copy_sums(k, 1)
+            times_one_plus_tanh(pair_a[1])
             if more:
                 for c in passes:
                     multiply(following, c)
@@ -334,7 +345,7 @@ def tile_dynamic_estimator_v_kernel(tc, x, mean, rho, quad, grad_out, out):
             if more:
                 for c in passes:
                     regroup_e(following, c)
-                column_sums(following)
+                column_sums(following, 0)
             for pair in round_pairs[LEAD_PAIRS:]:
                 rho_step(pair)
             if exp_turn and more:
@@ -355,7 +366,7 @@ def tile_dynamic_estimator_v_kernel(tc, x, mean, rho, quad, grad_out, out):
                 matmuls((first + CHUNK_TILES, first + CHUNK_TILES + 1))
             times_one_plus_tanh(pair_b[0])
             if more:
-                copy_sums(following)
+                copy_sums(following, 0)
             times_one_plus_tanh(pair_b[1])
             if exp_turn:
                 for i in round_tiles:

@@ -284,11 +284,11 @@ def tile_dynamic_estimator_v_kernel(tc, x, mean, rho, quad, grad_out, out):
             load_e(0, c)
         for c in passes:
             load_x(c, 1)
-        for c in passes:
-            load_e(1, c)
-        mean_rows[0] = load_class_rows(mean_pool, mean, 0)
         rho_rows[0] = load_class_rows(rho_pool, rho, 0)
         rho_rows[1] = load_class_rows(rho_pool, rho, 1)
+        mean_rows[0] = load_class_rows(mean_pool, mean, 0)
+        for c in passes:
+            load_e(1, c)
 
         for c in passes:
             quantise_x(c, 0)
@@ -303,10 +303,10 @@ def tile_dynamic_estimator_v_kernel(tc, x, mean, rho, quad, grad_out, out):
                 copy_sums(0, 0)
             quantise_x(c, 1)
         matmuls((0, 1))
-        for c in passes:
-            exponential(1, c)
         for i in range(ROUND_TILES):
             tanh_rho(i)
+        for c in passes:
+            exponential(1, c)
 
         for k in range(CHUNKS):
             first = k * CHUNK_TILES

@@ -52,8 +52,6 @@ def tile_dynamic_estimator_v_kernel(tc, x, mean, rho, quad, grad_out, out):
         p2_pool = psum_pool("p2", 4)
         s0_pool = psum_pool("s0", 1)
 
-        stack.enter_context(tc.manual_schedule())
-
         x_codes = keep.tile([P, PASSES, FEATURES], U32, align_bytes=64)
         x_scales = keep.tile([P, PASSES, FEATURES], U8, align_bytes=64)
         xx_codes = keep.tile([P, PASSES, FEATURES], U32, align_bytes=64)

@@ -23,6 +23,8 @@ FEATURE_HALVES = FEATURES // WIDTH
 RUN = 4
 ROUND_TILES = 2 * CHUNK_TILES
 LEAD_PAIRS = 1
+CLASS_TILES = CLASSES // P
+WORK_SLOTS = 9
 
 FLOPS = 2 * 2 * BATCH * CLASSES * FEATURES
 
@@ -39,14 +41,16 @@ def tile_dynamic_estimator_v_kernel(tc, x, mean, rho, quad, grad_out, out):
 
         keep = sbuf_pool("keep", 1)
         quad_pool = sbuf_pool("quad", 2 * PASSES)
-        rows_pool = sbuf_pool("rows", 6)
-        grouped_pool = sbuf_pool("grouped", 4)
+        grad_pool = sbuf_pool("grad", 2 * PASSES)
+        grouped_pool = sbuf_pool("grouped", 2)
+        work_pool = sbuf_pool("work", WORK_SLOTS)
         codes_pool = sbuf_pool("codes", 2)
         rho_pool = sbuf_pool("rho", 2)
         mean_pool = sbuf_pool("mean", 2)
         tanh_pool = sbuf_pool("tanh", ROUND_TILES)
         chain_pool = sbuf_pool("chain", ROUND_TILES)
-        acc_pool = sbuf_pool("acc", ROUND_TILES)
+        q_pool = sbuf_pool("q", 2)
+        a_pool = sbuf_pool("a", 2)
         sums_pool = sbuf_pool("sums", 2)
         p1_pool = psum_pool("p1", 3)
         p2_pool = psum_pool("p2", 4)
@@ -57,12 +61,17 @@ def tile_dynamic_estimator_v_kernel(tc, x, mean, rho, quad, grad_out, out):
         xx_codes = keep.tile([P, PASSES, FEATURES], U32, align_bytes=64)
         xx_scales = keep.tile([P, PASSES, FEATURES], U8, align_bytes=64)
         halves = keep.tile([P, P], F32)
-        nc.vector.memset(halves[:], 0.5)
+        nc.gpsimd.memset(halves[:], 0.5)
 
-        x_rows, e_rows, grad_rows, e_grouped = {}, {}, {}, {}
+        stack.enter_context(
+            tc.manual_schedule(engines={mybir.EngineType.Activation, mybir.EngineType.DVE})
+        )
+
+        x_rows, x_grouped, squared = {}, {}, {}
+        e_rows, grad_rows, e_grouped = {}, {}, {}
         e_codes, e_scales, half_s0, s0_bank = {}, {}, {}, {}
-        rho_rows, mean_rows, tanh_half, chain, acc = {}, {}, {}, {}, {}
-        p1, p2 = {}, {}
+        rho_rows, mean_rows, tanh_half, chain = {}, {}, {}, {}
+        p1, p2, q_tiles, a_tiles, y_tiles = {}, {}, {}, {}, {}
 
         def piece(index):
             return slice(index * WIDTH, (index + 1) * WIDTH)
@@ -74,19 +83,18 @@ def tile_dynamic_estimator_v_kernel(tc, x, mean, rho, quad, grad_out, out):
         def flat(grouped):
             return grouped[:].rearrange("p w j -> p (w j)")
 
-        def load_bf16_rows(source, c, cols):
-            rows = rows_pool.tile([P, PACK, WIDTH], BF16)
-            nc.sync.dma_start(out=rows[:], in_=batch_rows(source, c, cols))
-            return rows
-
         def load_x(c, h):
-            x_rows[c, h] = load_bf16_rows(x, c, piece(h))
+            rows = work_pool.tile([P, PACK, WIDTH], BF16, tag="work", align_bytes=64)
+            nc.sync.dma_start(out=rows[:], in_=batch_rows(x, c, piece(h)))
+            x_rows[c, h] = rows
 
         def load_e(k, c):
             quad_rows = quad_pool.tile([P, PACK, WIDTH], F32)
             nc.sync.dma_start(out=quad_rows[:], in_=batch_rows(quad, c, piece(k)))
             e_rows[k, c] = quad_rows
-            grad_rows[k, c] = load_bf16_rows(grad_out, c, piece(k))
+            rows = grad_pool.tile([P, PACK, WIDTH], BF16)
+            nc.sync.dma_start(out=rows[:], in_=batch_rows(grad_out, c, piece(k)))
+            grad_rows[k, c] = rows
 
         def load_class_rows(pool, source, k):
             class_rows = pool.tile([P, CHUNK_TILES, FEATURES], BF16)
@@ -101,32 +109,35 @@ def tile_dynamic_estimator_v_kernel(tc, x, mean, rho, quad, grad_out, out):
                 in_=rows[:, :, cols].rearrange("p j (w i) -> p w j i", i=RUN),
             )
 
-        def grouped_tile():
-            grouped = grouped_pool.tile([P, WIDTH, PACK], BF16, align_bytes=64)
-            return grouped
+        parts = (slice(0, WIDTH // 2), slice(WIDTH // 2, WIDTH))
 
-        def quantise_x(c, h):
-            x_grouped = grouped_tile()
-            squared = grouped_tile()
-            parts = (slice(0, WIDTH // 2), slice(WIDTH // 2, WIDTH))
+        def regroup_x(c, h):
+            grouped = work_pool.tile([P, WIDTH, PACK], BF16, tag="work", align_bytes=64)
+            x_grouped[c, h] = grouped
             for cols in parts:
-                regroup(nc.vector.tensor_copy, x_grouped, x_rows[c, h], cols)
+                regroup(nc.vector.tensor_copy, grouped, x_rows[c, h], cols)
+
+        def square_x(c, h):
+            product_tile = work_pool.tile([P, WIDTH, PACK], BF16, tag="work", align_bytes=64)
+            squared[c, h] = product_tile
             for cols in parts:
                 nc.vector.tensor_tensor(
-                    out=squared[:, cols, :],
-                    in0=x_grouped[:, cols, :],
-                    in1=x_grouped[:, cols, :],
+                    out=product_tile[:, cols, :],
+                    in0=x_grouped[c, h][:, cols, :],
+                    in1=x_grouped[c, h][:, cols, :],
                     op=ALU.mult,
                 )
+
+        def quantise_x(c, h):
             nc.vector.quantize_mx(
                 out=x_codes[:, c, piece(h)].bitcast(E4M3_X4),
                 scales=x_scales[:, c, piece(h)],
-                in_=flat(x_grouped),
+                in_=flat(x_grouped[c, h]),
             )
             nc.vector.quantize_mx(
                 out=xx_codes[:, c, piece(h)].bitcast(E4M3_X4),
                 scales=xx_scales[:, c, piece(h)],
-                in_=flat(squared),
+                in_=flat(squared[c, h]),
             )
 
         def exponential(k, c):
@@ -138,8 +149,10 @@ def tile_dynamic_estimator_v_kernel(tc, x, mean, rho, quad, grad_out, out):
             )
 
         def regroup_e(k, c):
-            e_grouped[k, c] = grouped_tile()
-            regroup(nc.scalar.copy, e_grouped[k, c], e_rows[k, c], slice(0, WIDTH))
+            grouped = grouped_pool.tile([P, WIDTH, PACK], BF16, align_bytes=64)
+            e_grouped[k, c] = grouped
+            copy = nc.scalar.copy if c == 0 else nc.vector.tensor_copy
+            regroup(copy, grouped, e_rows[k, c], slice(0, WIDTH))
 
         def quantise_e(k, c):
             if c == 0:
@@ -152,31 +165,25 @@ def tile_dynamic_estimator_v_kernel(tc, x, mean, rho, quad, grad_out, out):
                 in_=flat(e_grouped[k, c]),
             )
 
-        def pair_of_chunk(a):
-            return slice(2 * a, 2 * a + 2)
-
-        def column_sums(k, a):
-            if a == 0:
+        def column_sums(k, t):
+            if t == 0:
                 bank = s0_pool.tile([P, CHUNK_TILES, P], F32)
                 s0_bank[k] = bank
             slices = [(c, j) for c in range(PASSES) for j in range(PACK)]
-            for t in range(CHUNK_TILES)[pair_of_chunk(a)]:
-                for c, j in slices:
-                    nc.tensor.matmul(
-                        out=s0_bank[k][:, t, :],
-                        lhsT=e_rows[k, c][:, j, t * P : (t + 1) * P],
-                        rhs=halves[:],
-                        start=((c, j) == slices[0]),
-                        stop=((c, j) == slices[-1]),
-                    )
+            for c, j in slices:
+                nc.tensor.matmul(
+                    out=s0_bank[k][:, t, :],
+                    lhsT=e_rows[k, c][:, j, t * P : (t + 1) * P],
+                    rhs=halves[:],
+                    start=((c, j) == slices[0]),
+                    stop=((c, j) == slices[-1]),
+                )
 
-        def copy_sums(k, a):
-            if a == 0:
+        def copy_sums(k, t):
+            if t == 0:
                 sums = sums_pool.tile([P, CHUNK_TILES, 1], F32)
                 half_s0[k] = sums
-            nc.vector.tensor_copy(
-                out=half_s0[k][:, pair_of_chunk(a), :], in_=s0_bank[k][:, pair_of_chunk(a), 0:1]
-            )
+            nc.vector.tensor_copy(out=half_s0[k][:, t, :], in_=s0_bank[k][:, t, 0:1])
 
         def tanh_rho(i):
             k, t = divmod(i, CHUNK_TILES)
@@ -218,17 +225,17 @@ def tile_dynamic_estimator_v_kernel(tc, x, mean, rho, quad, grad_out, out):
                     stop=(c == PASSES - 1),
                 )
 
-        def matmuls(pair):
-            for i in pair:
-                for h in range(FEATURE_HALVES):
-                    p1_bank = p1_pool.tile([P, WIDTH], F32)
-                    product(p1_bank, i, x_codes, x_scales, h)
-                    p1[i, h] = p1_bank
-            for i in pair:
-                for h in range(FEATURE_HALVES):
-                    p2_bank = p2_pool.tile([P, WIDTH], F32)
-                    product(p2_bank, i, xx_codes, xx_scales, h)
-                    p2[i, h] = p2_bank
+        def first_moment(i):
+            for h in range(FEATURE_HALVES):
+                p1_bank = p1_pool.tile([P, WIDTH], F32)
+                product(p1_bank, i, x_codes, x_scales, h)
+                p1[i, h] = p1_bank
+
+        def second_moment(i):
+            for h in range(FEATURE_HALVES):
+                p2_bank = p2_pool.tile([P, WIDTH], F32)
+                product(p2_bank, i, xx_codes, xx_scales, h)
+                p2[i, h] = p2_bank
 
         def mean_tile(i):
             k, t = divmod(i, CHUNK_TILES)
@@ -236,136 +243,174 @@ def tile_dynamic_estimator_v_kernel(tc, x, mean, rho, quad, grad_out, out):
 
         def mean_s0_minus_p1(i):
             k, t = divmod(i, CHUNK_TILES)
-            acc_tile = acc_pool.tile([P, FEATURES], F32)
+            q_tile = q_pool.tile([P, FEATURES], F32)
             for h in range(FEATURE_HALVES):
                 nc.vector.scalar_tensor_tensor(
-                    out=acc_tile[:, piece(h)],
+                    out=q_tile[:, piece(h)],
                     in0=mean_tile(i)[:, piece(h)],
                     scalar=half_s0[k][:, t, :],
                     in1=p1[i, h][:],
                     op0=ALU.mult,
                     op1=ALU.subtract,
                 )
-            acc[i] = acc_tile
+            q_tiles[i] = q_tile
 
         def times_mean(i):
-            nc.vector.tensor_tensor(out=acc[i][:], in0=acc[i][:], in1=mean_tile(i), op=ALU.mult)
+            a_tile = a_pool.tile([P, FEATURES], F32)
+            nc.gpsimd.tensor_tensor(out=a_tile[:], in0=q_tiles[i][:], in1=mean_tile(i), op=ALU.mult)
+            a_tiles[i] = a_tile
 
         def plus_half_p2(i):
             for h in range(FEATURE_HALVES):
                 nc.vector.scalar_tensor_tensor(
-                    out=acc[i][:, piece(h)],
+                    out=a_tiles[i][:, piece(h)],
                     in0=p2[i, h][:],
                     scalar=0.5,
-                    in1=acc[i][:, piece(h)],
+                    in1=a_tiles[i][:, piece(h)],
                     op0=ALU.mult,
                     op1=ALU.add,
                 )
 
         def times_one_plus_tanh(i):
+            y_tile = work_pool.tile([P, FEATURES], F32, tag="work", align_bytes=64)
             nc.vector.scalar_tensor_tensor(
-                out=acc[i][:],
+                out=y_tile[:],
                 in0=tanh_half[i][:],
                 scalar=1.0,
-                in1=acc[i][:],
+                in1=a_tiles[i][:],
                 op0=ALU.add,
                 op1=ALU.mult,
             )
+            y_tiles[i] = y_tile
 
         def finish(i):
-            nc.vector.tensor_tensor(out=acc[i][:], in0=acc[i][:], in1=chain[i][:], op=ALU.mult)
-            nc.sync.dma_start(out=out[i * P : (i + 1) * P, :], in_=acc[i][:])
+            nc.vector.tensor_tensor(
+                out=y_tiles[i][:], in0=y_tiles[i][:], in1=chain[i][:], op=ALU.mult
+            )
+            nc.sync.dma_start(out=out[i * P : (i + 1) * P, :], in_=y_tiles[i][:])
 
-        passes = range(PASSES)
-        for c in passes:
-            load_x(c, 0)
-            load_e(0, c)
-        for c in passes:
-            load_x(c, 1)
+        load_x(0, 0)
+        load_x(1, 0)
+        load_e(0, 0)
+        load_e(0, 1)
+        load_x(0, 1)
+        load_x(1, 1)
         rho_rows[0] = load_class_rows(rho_pool, rho, 0)
         rho_rows[1] = load_class_rows(rho_pool, rho, 1)
+        load_e(1, 0)
         mean_rows[0] = load_class_rows(mean_pool, mean, 0)
-        for c in passes:
-            load_e(1, c)
+        load_e(1, 1)
 
-        for c in passes:
+        for c in range(PASSES):
+            regroup_x(c, 0)
+            square_x(c, 0)
             quantise_x(c, 0)
+        for c in range(PASSES):
             exponential(0, c)
             multiply(0, c)
-        for c in passes:
-            regroup_e(0, c)
-        column_sums(0, 0)
-        for c in passes:
-            quantise_e(0, c)
-            if c == PASSES - 1:
-                copy_sums(0, 0)
-            quantise_x(c, 1)
-        matmuls((0, 1))
-        for i in range(ROUND_TILES):
+        regroup_e(0, 0)
+        for t in range(CHUNK_TILES):
+            column_sums(0, t)
+        regroup_x(0, 1)
+        regroup_e(0, 1)
+        square_x(0, 1)
+        quantise_e(0, 0)
+        quantise_x(0, 1)
+        quantise_e(0, 1)
+        regroup_x(1, 1)
+        square_x(1, 1)
+        copy_sums(0, 0)
+        copy_sums(0, 1)
+        quantise_x(1, 1)
+        first_moment(0)
+        first_moment(1)
+        for i in range(0, 4):
             tanh_rho(i)
-        for c in passes:
-            exponential(1, c)
+        exponential(1, 0)
+        for i in range(4, 8):
+            tanh_rho(i)
+        exponential(1, 1)
+        for c in range(PASSES):
+            load_e(2, c)
+        mean_rows[1] = load_class_rows(mean_pool, mean, 1)
 
-        for k in range(CHUNKS):
-            first = k * CHUNK_TILES
-            pair_a, pair_b = (first, first + 1), (first + 2, first + 3)
-            following = k + 1
-            more = following < CHUNKS
-            exp_turn = k % 2 == 1
-            round_start = (k // 2) * ROUND_TILES
-            round_tiles = list(range(round_start, round_start + ROUND_TILES))
-            round_pairs = [(i, i + 1) for i in round_tiles[::2]]
-            rho_step = inverse_cubes if exp_turn else logarithms
+        last = CLASS_TILES - 1
+        for s in range(-2, CLASS_TILES):
+            if s == -2:
+                multiply(1, 0)
+                regroup_e(1, 0)
+            if s < 0:
+                copy_sums(0, s + 4)
+            if s >= 0:
+                plus_half_p2(s)
+            if s + 2 <= last:
+                mean_s0_minus_p1(s + 2)
+            if 0 <= s + 1 <= last:
+                times_mean(s + 1)
 
-            if k + 2 < CHUNKS:
-                for c in passes:
-                    load_e(k + 2, c)
-                rho_rows[k + 2] = load_class_rows(rho_pool, rho, k + 2)
-            if more:
-                mean_rows[following] = load_class_rows(mean_pool, mean, following)
+            following, phase = divmod(s + 6, CHUNK_TILES)
+            if 1 <= following < CHUNKS and s >= -1:
+                if phase == 0:
+                    multiply(following, 0)
+                    regroup_e(following, 0)
+                if phase == 1:
+                    multiply(following, 1)
+                if phase == 2:
+                    regroup_e(following, 1)
+                    quantise_e(following, 0)
+                if phase == 3:
+                    quantise_e(following, 1)
+            sums_chunk, sums_tile = divmod(s + 3, CHUNK_TILES)
+            if 1 <= sums_chunk < CHUNKS:
+                copy_sums(sums_chunk, sums_tile)
 
-            if exp_turn and more:
-                for c in passes:
-                    exponential(following, c)
-            column_sums(k, 1)
-            matmuls(pair_b)
-            for step in (mean_s0_minus_p1, times_mean, plus_half_p2):
-                for i in pair_a:
-                    step(i)
-            times_one_plus_tanh(pair_a[0])
-            copy_sums(k, 1)
-            times_one_plus_tanh(pair_a[1])
-            if more:
-                for c in passes:
-                    multiply(following, c)
-            for pair in round_pairs[:LEAD_PAIRS]:
-                rho_step(pair)
-            if more:
-                for c in passes:
-                    regroup_e(following, c)
-                column_sums(following, 0)
-            for pair in round_pairs[LEAD_PAIRS:]:
-                rho_step(pair)
-            if exp_turn and more:
-                for c in passes:
-                    exponential(following + 1, c)
-                for i in round_tiles:
-                    tanh_rho(i + ROUND_TILES)
+            if s == -2:
+                for c in range(PASSES):
+                    exponential(2, c)
+            if s in (-1, 0, 2, 3):
+                first = 2 * (s + 1) if s < 2 else 2 * s
+                logarithms((first, first + 1))
+            if s == 2:
+                rho_rows[2] = load_class_rows(rho_pool, rho, 2)
+                rho_rows[3] = load_class_rows(rho_pool, rho, 3)
+            if s == 4:
+                for c in range(PASSES):
+                    load_e(3, c)
+                mean_rows[2] = load_class_rows(mean_pool, mean, 2)
+                for c in range(PASSES):
+                    exponential(3, c)
+                inverse_cubes((0, 1))
+            if s == 5:
+                inverse_cubes((2, 3))
+                tanh_rho(8)
+                tanh_rho(9)
+            if s == 6:
+                tanh_rho(10)
+                tanh_rho(11)
+                inverse_cubes((4, 5))
+            if s == 7:
+                inverse_cubes((6, 7))
+                for i in range(12, 16):
+                    tanh_rho(i)
+            if s == 8:
+                mean_rows[3] = load_class_rows(mean_pool, mean, 3)
+            if 8 <= s <= 11:
+                logarithms((2 * s - 8, 2 * s - 7))
+            if 12 <= s <= 15:
+                inverse_cubes((2 * s - 16, 2 * s - 15))
 
-            for i in pair_b:
-                mean_s0_minus_p1(i)
-            if more:
-                quantise_e(following, 0)
-            for step in (times_mean, plus_half_p2):
-                for i in pair_b:
-                    step(i)
-            if more:
-                quantise_e(following, 1)
-                matmuls((first + CHUNK_TILES, first + CHUNK_TILES + 1))
-            times_one_plus_tanh(pair_b[0])
-            if more:
-                copy_sums(following, 0)
-            times_one_plus_tanh(pair_b[1])
-            if exp_turn:
-                for i in round_tiles:
-                    finish(i)
+            if 7 <= s <= 10:
+                finish(2 * s - 14)
+                finish(2 * s - 13)
+            if s >= 0:
+                times_one_plus_tanh(s)
+
+            if 0 <= s + 1 <= last:
+                second_moment(s + 1)
+            if 2 <= s + 3 <= last:
+                first_moment(s + 3)
+            sums_chunk, sums_tile = divmod(s + 4, CHUNK_TILES)
+            if 1 <= sums_chunk < CHUNKS:
+                column_sums(sums_chunk, sums_tile)
+        for i in range(ROUND_TILES, CLASS_TILES):
+            finish(i)

@@ -256,31 +256,38 @@ def tile_dynamic_estimator_v_kernel(tc, x, mean, rho, quad, grad_out, out):
             q_tiles[i] = q_tile
 
         def times_mean(i):
-            a_tile = a_pool.tile([P, FEATURES], F32)
-            nc.gpsimd.tensor_tensor(out=a_tile[:], in0=q_tiles[i][:], in1=mean_tile(i), op=ALU.mult)
-            a_tiles[i] = a_tile
+            for h in range(FEATURE_HALVES):
+                a_tile = a_pool.tile([P, WIDTH], F32, tag="a%d" % h)
+                nc.gpsimd.tensor_tensor(
+                    out=a_tile[:],
+                    in0=q_tiles[i][:, piece(h)],
+                    in1=mean_tile(i)[:, piece(h)],
+                    op=ALU.mult,
+                )
+                a_tiles[i, h] = a_tile
 
         def plus_half_p2(i):
             for h in range(FEATURE_HALVES):
                 nc.vector.scalar_tensor_tensor(
-                    out=a_tiles[i][:, piece(h)],
+                    out=a_tiles[i, h][:],
                     in0=p2[i, h][:],
                     scalar=0.5,
-                    in1=a_tiles[i][:, piece(h)],
+                    in1=a_tiles[i, h][:],
                     op0=ALU.mult,
                     op1=ALU.add,
                 )
 
         def times_one_plus_tanh(i):
             y_tile = work_pool.tile([P, FEATURES], F32, tag="work", align_bytes=64)
-            nc.vector.scalar_tensor_tensor(
-                out=y_tile[:],
-                in0=tanh_half[i][:],
-                scalar=1.0,
-                in1=a_tiles[i][:],
-                op0=ALU.add,
-                op1=ALU.mult,
-            )
+            for h in range(FEATURE_HALVES):
+                nc.vector.scalar_tensor_tensor(
+                    out=y_tile[:, piece(h)],
+                    in0=tanh_half[i][:, piece(h)],
+                    scalar=1.0,
+                    in1=a_tiles[i, h][:],
+                    op0=ALU.add,
+                    op1=ALU.mult,
+                )
             y_tiles[i] = y_tile
 
         def finish(i):

@@ -24,7 +24,7 @@ RUN = 4
 ROUND_TILES = 2 * CHUNK_TILES
 LEAD_PAIRS = 1
 CLASS_TILES = CLASSES // P
-WORK_SLOTS = 9
+WORK_SLOTS = 8
 
 FLOPS = 2 * 2 * BATCH * CLASSES * FEATURES
 
@@ -51,6 +51,7 @@ def tile_dynamic_estimator_v_kernel(tc, x, mean, rho, quad, grad_out, out):
         chain_pool = sbuf_pool("chain", ROUND_TILES)
         q_pool = sbuf_pool("q", 2)
         a_pool = sbuf_pool("a", 2)
+        b_pool = sbuf_pool("b", 2)
         sums_pool = sbuf_pool("sums", 2)
         p1_pool = psum_pool("p1", 3)
         p2_pool = psum_pool("p2", 4)
@@ -71,7 +72,7 @@ def tile_dynamic_estimator_v_kernel(tc, x, mean, rho, quad, grad_out, out):
         e_rows, grad_rows, e_grouped = {}, {}, {}
         e_codes, e_scales, half_s0, s0_bank = {}, {}, {}, {}
         rho_rows, mean_rows, tanh_half, chain = {}, {}, {}, {}
-        p1, p2, q_tiles, a_tiles, y_tiles = {}, {}, {}, {}, {}
+        p1, p2, q_tiles, a_tiles, v_halves, y_tiles = {}, {}, {}, {}, {}, {}
 
         def piece(index):
             return slice(index * WIDTH, (index + 1) * WIDTH)
@@ -256,23 +257,19 @@ def tile_dynamic_estimator_v_kernel(tc, x, mean, rho, quad, grad_out, out):
             q_tiles[i] = q_tile
 
         def times_mean(i):
-            for h in range(FEATURE_HALVES):
-                a_tile = a_pool.tile([P, WIDTH], F32, tag="a%d" % h)
-                nc.gpsimd.tensor_tensor(
-                    out=a_tile[:],
-                    in0=q_tiles[i][:, piece(h)],
-                    in1=mean_tile(i)[:, piece(h)],
-                    op=ALU.mult,
-                )
-                a_tiles[i, h] = a_tile
+            a_tile = a_pool.tile([P, FEATURES], F32)
+            nc.gpsimd.tensor_tensor(out=a_tile[:], in0=q_tiles[i][:], in1=mean_tile(i), op=ALU.mult)
+            a_tiles[i] = a_tile
 
         def plus_half_p2(i):
+            b_tile = b_pool.tile([P, WIDTH], F32)
+            v_halves[i] = (a_tiles[i][:, piece(0)], b_tile[:])
             for h in range(FEATURE_HALVES):
                 nc.vector.scalar_tensor_tensor(
-                    out=a_tiles[i, h][:],
+                    out=v_halves[i][h],
                     in0=p2[i, h][:],
                     scalar=0.5,
-                    in1=a_tiles[i, h][:],
+                    in1=a_tiles[i][:, piece(h)],
                     op0=ALU.mult,
                     op1=ALU.add,
                 )
@@ -284,7 +281,7 @@ def tile_dynamic_estimator_v_kernel(tc, x, mean, rho, quad, grad_out, out):
                     out=y_tile[:, piece(h)],
                     in0=tanh_half[i][:, piece(h)],
                     scalar=1.0,
-                    in1=a_tiles[i, h][:],
+                    in1=v_halves[i][h],
                     op0=ALU.add,
                     op1=ALU.mult,
                 )

@@ -25,6 +25,7 @@ ROUND_TILES = 2 * CHUNK_TILES
 LEAD_PAIRS = 1
 CLASS_TILES = CLASSES // P
 WORK_SLOTS = 8
+FIRST_SPLIT_TILE = 11
 
 FLOPS = 2 * 2 * BATCH * CLASSES * FEATURES
 
@@ -42,7 +43,7 @@ def tile_dynamic_estimator_v_kernel(tc, x, mean, rho, quad, grad_out, out):
         keep = sbuf_pool("keep", 1)
         quad_pool = sbuf_pool("quad", 2 * PASSES)
         grad_pool = sbuf_pool("grad", 2 * PASSES)
-        grouped_pool = sbuf_pool("grouped", 2)
+        grouped_pool = sbuf_pool("grouped", 1)
         work_pool = sbuf_pool("work", WORK_SLOTS)
         codes_pool = sbuf_pool("codes", 2)
         rho_pool = sbuf_pool("rho", 2)
@@ -104,30 +105,32 @@ def tile_dynamic_estimator_v_kernel(tc, x, mean, rho, quad, grad_out, out):
             )
             return class_rows
 
-        def regroup(copy, grouped, rows, cols):
+        def regroup(copy, grouped, rows):
             copy(
-                out=grouped[:, cols, :].rearrange("p (w i) j -> p w j i", i=RUN),
-                in_=rows[:, :, cols].rearrange("p j (w i) -> p w j i", i=RUN),
+                out=grouped.rearrange("p (w i) j -> p w j i", i=RUN),
+                in_=rows.rearrange("p j (w i) -> p w j i", i=RUN),
             )
-
-        parts = (slice(0, WIDTH // 2), slice(WIDTH // 2, WIDTH))
 
         def regroup_x(c, h):
             grouped = work_pool.tile([P, WIDTH, PACK], BF16, tag="work", align_bytes=64)
             x_grouped[c, h] = grouped
-            for cols in parts:
-                regroup(nc.vector.tensor_copy, grouped, x_rows[c, h], cols)
+            regroup(nc.vector.tensor_copy, grouped[:], x_rows[c, h][:])
 
         def square_x(c, h):
             product_tile = work_pool.tile([P, WIDTH, PACK], BF16, tag="work", align_bytes=64)
             squared[c, h] = product_tile
-            for cols in parts:
-                nc.vector.tensor_tensor(
-                    out=product_tile[:, cols, :],
-                    in0=x_grouped[c, h][:, cols, :],
-                    in1=x_grouped[c, h][:, cols, :],
-                    op=ALU.mult,
-                )
+            nc.vector.tensor_tensor(
+                out=product_tile[:], in0=x_grouped[c, h][:], in1=x_grouped[c, h][:], op=ALU.mult
+            )
+
+        def square_x_on_scalar(c, h):
+            product_tile = work_pool.tile([P, WIDTH, PACK], BF16, tag="work", align_bytes=64)
+            squared[c, h] = product_tile
+            nc.scalar.activation(
+                out=product_tile[:].rearrange("p (w i) j -> p w j i", i=RUN),
+                in_=x_rows[c, h][:].rearrange("p j (w i) -> p w j i", i=RUN),
+                func=ACT.Square,
+            )
 
         def quantise_x(c, h):
             nc.vector.quantize_mx(
@@ -135,6 +138,8 @@ def tile_dynamic_estimator_v_kernel(tc, x, mean, rho, quad, grad_out, out):
                 scales=x_scales[:, c, piece(h)],
                 in_=flat(x_grouped[c, h]),
             )
+
+        def quantise_square(c, h):
             nc.vector.quantize_mx(
                 out=xx_codes[:, c, piece(h)].bitcast(E4M3_X4),
                 scales=xx_scales[:, c, piece(h)],
@@ -150,20 +155,20 @@ def tile_dynamic_estimator_v_kernel(tc, x, mean, rho, quad, grad_out, out):
             )
 
         def regroup_e(k, c):
-            grouped = grouped_pool.tile([P, WIDTH, PACK], BF16, align_bytes=64)
-            e_grouped[k, c] = grouped
-            copy = nc.scalar.copy if c == 0 else nc.vector.tensor_copy
-            regroup(copy, grouped, e_rows[k, c], slice(0, WIDTH))
-
-        def quantise_e(k, c):
             if c == 0:
-                codes = codes_pool.tile([P, PASSES, WIDTH], U32, align_bytes=64)
-                scales = codes_pool.tile([P, PASSES, WIDTH], U8, align_bytes=64)
-                e_codes[k], e_scales[k] = codes, scales
+                grouped = grouped_pool.tile([P, PASSES, WIDTH, PACK], BF16, align_bytes=64)
+                e_grouped[k] = grouped
+            copy = nc.scalar.copy if c == 0 else nc.vector.tensor_copy
+            regroup(copy, e_grouped[k][:, c, :, :], e_rows[k, c][:])
+
+        def quantise_e(k):
+            codes = codes_pool.tile([P, PASSES, WIDTH], U32, align_bytes=64)
+            scales = codes_pool.tile([P, PASSES, WIDTH], U8, align_bytes=64)
+            e_codes[k], e_scales[k] = codes, scales
             nc.vector.quantize_mx(
-                out=e_codes[k][:, c, :].bitcast(E5M2_X4),
-                scales=e_scales[k][:, c, :],
-                in_=flat(e_grouped[k, c]),
+                out=codes[:].rearrange("p c w -> p (c w)").bitcast(E5M2_X4),
+                scales=scales[:].rearrange("p c w -> p (c w)"),
+                in_=e_grouped[k][:].rearrange("p c w j -> p (c w j)"),
             )
 
         def column_sums(k, t):
@@ -180,11 +185,12 @@ def tile_dynamic_estimator_v_kernel(tc, x, mean, rho, quad, grad_out, out):
                     stop=((c, j) == slices[-1]),
                 )
 
-        def copy_sums(k, t):
-            if t == 0:
+        def copy_sums(k, a):
+            if a == 0:
                 sums = sums_pool.tile([P, CHUNK_TILES, 1], F32)
                 half_s0[k] = sums
-            nc.vector.tensor_copy(out=half_s0[k][:, t, :], in_=s0_bank[k][:, t, 0:1])
+            pair = slice(2 * a, 2 * a + 2)
+            nc.vector.tensor_copy(out=half_s0[k][:, pair, :], in_=s0_bank[k][:, pair, 0:1])
 
         def tanh_rho(i):
             k, t = divmod(i, CHUNK_TILES)
@@ -262,8 +268,11 @@ def tile_dynamic_estimator_v_kernel(tc, x, mean, rho, quad, grad_out, out):
             a_tiles[i] = a_tile
 
         def plus_half_p2(i):
-            b_tile = b_pool.tile([P, WIDTH], F32)
-            v_halves[i] = (a_tiles[i][:, piece(0)], b_tile[:])
+            if i < FIRST_SPLIT_TILE:
+                v_halves[i] = (a_tiles[i][:, piece(0)], a_tiles[i][:, piece(1)])
+            else:
+                b_tile = b_pool.tile([P, WIDTH], F32)
+                v_halves[i] = (a_tiles[i][:, piece(0)], b_tile[:])
             for h in range(FEATURE_HALVES):
                 nc.vector.scalar_tensor_tensor(
                     out=v_halves[i][h],
@@ -276,15 +285,25 @@ def tile_dynamic_estimator_v_kernel(tc, x, mean, rho, quad, grad_out, out):
 
         def times_one_plus_tanh(i):
             y_tile = work_pool.tile([P, FEATURES], F32, tag="work", align_bytes=64)
-            for h in range(FEATURE_HALVES):
+            if i < FIRST_SPLIT_TILE:
                 nc.vector.scalar_tensor_tensor(
-                    out=y_tile[:, piece(h)],
-                    in0=tanh_half[i][:, piece(h)],
+                    out=y_tile[:],
+                    in0=tanh_half[i][:],
                     scalar=1.0,
-                    in1=v_halves[i][h],
+                    in1=a_tiles[i][:],
                     op0=ALU.add,
                     op1=ALU.mult,
                 )
+            else:
+                for h in range(FEATURE_HALVES):
+                    nc.vector.scalar_tensor_tensor(
+                        out=y_tile[:, piece(h)],
+                        in0=tanh_half[i][:, piece(h)],
+                        scalar=1.0,
+                        in1=v_halves[i][h],
+                        op0=ALU.add,
+                        op1=ALU.mult,
+                    )
             y_tiles[i] = y_tile
 
         def finish(i):
@@ -305,10 +324,14 @@ def tile_dynamic_estimator_v_kernel(tc, x, mean, rho, quad, grad_out, out):
         mean_rows[0] = load_class_rows(mean_pool, mean, 0)
         load_e(1, 1)
 
-        for c in range(PASSES):
-            regroup_x(c, 0)
-            square_x(c, 0)
-            quantise_x(c, 0)
+        square_x_on_scalar(0, 0)
+        regroup_x(0, 0)
+        regroup_x(1, 0)
+        quantise_x(0, 0)
+        square_x(1, 0)
+        quantise_square(0, 0)
+        quantise_x(1, 0)
+        quantise_square(1, 0)
         for c in range(PASSES):
             exponential(0, c)
             multiply(0, c)
@@ -318,14 +341,14 @@ def tile_dynamic_estimator_v_kernel(tc, x, mean, rho, quad, grad_out, out):
         regroup_x(0, 1)
         regroup_e(0, 1)
         square_x(0, 1)
-        quantise_e(0, 0)
-        quantise_x(0, 1)
-        quantise_e(0, 1)
         regroup_x(1, 1)
+        quantise_x(0, 1)
+        quantise_e(0)
         square_x(1, 1)
-        copy_sums(0, 0)
-        copy_sums(0, 1)
+        quantise_square(0, 1)
         quantise_x(1, 1)
+        copy_sums(0, 0)
+        quantise_square(1, 1)
         first_moment(0)
         first_moment(1)
         for i in range(0, 4):
@@ -343,14 +366,20 @@ def tile_dynamic_estimator_v_kernel(tc, x, mean, rho, quad, grad_out, out):
             if s == -2:
                 multiply(1, 0)
                 regroup_e(1, 0)
-            if s < 0:
-                copy_sums(0, s + 4)
             if s >= 0:
                 plus_half_p2(s)
             if s + 2 <= last:
                 mean_s0_minus_p1(s + 2)
             if 0 <= s + 1 <= last:
                 times_mean(s + 1)
+            if (s + 3) % CHUNK_TILES == 0 and 1 <= (s + 3) // CHUNK_TILES < CHUNKS:
+                copy_sums((s + 3) // CHUNK_TILES, 0)
+            if (s + 1) % CHUNK_TILES == 0 and (s + 1) // CHUNK_TILES < CHUNKS:
+                copy_sums((s + 1) // CHUNK_TILES, 1)
+
+            late_results = 7 <= s <= 10
+            if 0 <= s < FIRST_SPLIT_TILE and not late_results:
+                times_one_plus_tanh(s)
 
             following, phase = divmod(s + 6, CHUNK_TILES)
             if 1 <= following < CHUNKS and s >= -1:
@@ -361,12 +390,8 @@ def tile_dynamic_estimator_v_kernel(tc, x, mean, rho, quad, grad_out, out):
                     multiply(following, 1)
                 if phase == 2:
                     regroup_e(following, 1)
-                    quantise_e(following, 0)
                 if phase == 3:
-                    quantise_e(following, 1)
-            sums_chunk, sums_tile = divmod(s + 3, CHUNK_TILES)
-            if 1 <= sums_chunk < CHUNKS:
-                copy_sums(sums_chunk, sums_tile)
+                    quantise_e(following)
 
             if s == -2:
                 for c in range(PASSES):
@@ -403,17 +428,18 @@ def tile_dynamic_estimator_v_kernel(tc, x, mean, rho, quad, grad_out, out):
             if 12 <= s <= 15:
                 inverse_cubes((2 * s - 16, 2 * s - 15))
 
-            if 7 <= s <= 10:
+            if late_results:
                 finish(2 * s - 14)
+                times_one_plus_tanh(s)
                 finish(2 * s - 13)
-            if s >= 0:
+            if s >= FIRST_SPLIT_TILE:
                 times_one_plus_tanh(s)
 
             if 0 <= s + 1 <= last:
                 second_moment(s + 1)
             if 2 <= s + 3 <= last:
                 first_moment(s + 3)
-            sums_chunk, sums_tile = divmod(s + 4, CHUNK_TILES)
+            sums_chunk, sums_tile = divmod(s + 5, CHUNK_TILES)
             if 1 <= sums_chunk < CHUNKS:
                 column_sums(sums_chunk, sums_tile)
         for i in range(ROUND_TILES, CLASS_TILES):

@@ -372,10 +372,6 @@ def tile_dynamic_estimator_v_kernel(tc, x, mean, rho, quad, grad_out, out):
                 mean_s0_minus_p1(s + 2)
             if 0 <= s + 1 <= last:
                 times_mean(s + 1)
-            if (s + 3) % CHUNK_TILES == 0 and 1 <= (s + 3) // CHUNK_TILES < CHUNKS:
-                copy_sums((s + 3) // CHUNK_TILES, 0)
-            if (s + 1) % CHUNK_TILES == 0 and (s + 1) // CHUNK_TILES < CHUNKS:
-                copy_sums((s + 1) // CHUNK_TILES, 1)
 
             late_results = 7 <= s <= 10
             if 0 <= s < FIRST_SPLIT_TILE and not late_results:
@@ -434,6 +430,11 @@ def tile_dynamic_estimator_v_kernel(tc, x, mean, rho, quad, grad_out, out):
                 finish(2 * s - 13)
             if s >= FIRST_SPLIT_TILE:
                 times_one_plus_tanh(s)
+
+            if (s + 3) % CHUNK_TILES == 0 and 1 <= (s + 3) // CHUNK_TILES < CHUNKS:
+                copy_sums((s + 3) // CHUNK_TILES, 0)
+            if (s + 1) % CHUNK_TILES == 0 and (s + 1) // CHUNK_TILES < CHUNKS:
+                copy_sums((s + 1) // CHUNK_TILES, 1)
 
             if 0 <= s + 1 <= last:
                 second_moment(s + 1)

@@ -1,6 +1,7 @@
 from contextlib import ExitStack
 
 import concourse.mybir as mybir
+from concourse.masks import make_identity
 
 F32 = mybir.dt.float32
 BF16 = mybir.dt.bfloat16
@@ -25,6 +26,9 @@ ROUND_TILES = 2 * CHUNK_TILES
 LEAD_PAIRS = 1
 CLASS_TILES = CLASSES // P
 WORK_SLOTS = 8
+SUM_COLUMNS = 64
+VECTOR_REGROUPS = (3,)
+VECTOR_ROWS = 3
 FIRST_SPLIT_TILE = 11
 
 FLOPS = 2 * 2 * BATCH * CLASSES * FEATURES
@@ -54,23 +58,33 @@ def tile_dynamic_estimator_v_kernel(tc, x, mean, rho, quad, grad_out, out):
         a_pool = sbuf_pool("a", 2)
         b_pool = sbuf_pool("b", 2)
         sums_pool = sbuf_pool("sums", 2)
-        p1_pool = psum_pool("p1", 3)
-        p2_pool = psum_pool("p2", 4)
+        p1_pool = psum_pool("p1", 2)
+        p2_pool = psum_pool("p2", 2)
+        g_pool = psum_pool("g", VECTOR_ROWS)
         s0_pool = psum_pool("s0", 1)
 
         x_codes = keep.tile([P, PASSES, FEATURES], U32, align_bytes=64)
         x_scales = keep.tile([P, PASSES, FEATURES], U8, align_bytes=64)
         xx_codes = keep.tile([P, PASSES, FEATURES], U32, align_bytes=64)
         xx_scales = keep.tile([P, PASSES, FEATURES], U8, align_bytes=64)
-        halves = keep.tile([P, P], F32)
+        halves = keep.tile([P, SUM_COLUMNS], F32)
         nc.gpsimd.memset(halves[:], 0.5)
+        identity = keep.tile([P, P], BF16)
+        make_identity(nc, identity[:])
 
         stack.enter_context(
-            tc.manual_schedule(engines={mybir.EngineType.Activation, mybir.EngineType.DVE})
+            tc.manual_schedule(
+                engines={
+                    mybir.EngineType.Activation,
+                    mybir.EngineType.DVE,
+                    mybir.EngineType.PE,
+                    mybir.EngineType.Pool,
+                }
+            )
         )
 
         x_rows, x_grouped, squared = {}, {}, {}
-        e_rows, grad_rows, e_grouped = {}, {}, {}
+        e_rows, grad_rows, grad_banks, e_grouped = {}, {}, {}, {}
         e_codes, e_scales, half_s0, s0_bank = {}, {}, {}, {}
         rho_rows, mean_rows, tanh_half, chain = {}, {}, {}, {}
         p1, p2, q_tiles, a_tiles, v_halves, y_tiles = {}, {}, {}, {}, {}, {}
@@ -85,18 +99,29 @@ def tile_dynamic_estimator_v_kernel(tc, x, mean, rho, quad, grad_out, out):
         def flat(grouped):
             return grouped[:].rearrange("p w j -> p (w j)")
 
+        def exp_parts(k):
+            return (slice(0, 2), slice(2, 4)) if k == 0 else (slice(0, 4),)
+
         def load_x(c, h):
             rows = work_pool.tile([P, PACK, WIDTH], BF16, tag="work", align_bytes=64)
             nc.sync.dma_start(out=rows[:], in_=batch_rows(x, c, piece(h)))
             x_rows[c, h] = rows
 
-        def load_e(k, c):
+        def load_quad(k, c):
             quad_rows = quad_pool.tile([P, PACK, WIDTH], F32)
-            nc.sync.dma_start(out=quad_rows[:], in_=batch_rows(quad, c, piece(k)))
+            source = batch_rows(quad, c, piece(k))
+            for rows in exp_parts(k):
+                nc.sync.dma_start(out=quad_rows[:, rows, :], in_=source[:, rows, :])
             e_rows[k, c] = quad_rows
+
+        def load_grad(k, c):
             rows = grad_pool.tile([P, PACK, WIDTH], BF16)
             nc.sync.dma_start(out=rows[:], in_=batch_rows(grad_out, c, piece(k)))
             grad_rows[k, c] = rows
+
+        def load_e(k, c):
+            load_quad(k, c)
+            load_grad(k, c)
 
         def load_class_rows(pool, source, k):
             class_rows = pool.tile([P, CHUNK_TILES, FEATURES], BF16)
@@ -147,18 +172,49 @@ def tile_dynamic_estimator_v_kernel(tc, x, mean, rho, quad, grad_out, out):
             )
 
         def exponential(k, c):
-            nc.scalar.activation(out=e_rows[k, c][:], in_=e_rows[k, c][:], func=ACT.Exp, scale=-1.0)
+            for rows in exp_parts(k):
+                e_part = e_rows[k, c][:, rows, :]
+                nc.scalar.activation(out=e_part, in_=e_part, func=ACT.Exp, scale=-1.0)
+
+        def copy_grad(k, c, count):
+            for j in range(count):
+                g_bank = g_pool.tile([P, WIDTH], F32)
+                nc.tensor.matmul(
+                    out=g_bank[:],
+                    lhsT=identity[:],
+                    rhs=grad_rows[k, c][:, j, :],
+                    start=True,
+                    stop=True,
+                )
+                grad_banks[k, c, j] = g_bank
 
         def multiply(k, c):
             nc.vector.tensor_tensor(
                 out=e_rows[k, c][:], in0=e_rows[k, c][:], in1=grad_rows[k, c][:], op=ALU.mult
             )
 
+        def multiply_from_psum(k, c, count):
+            for j in range(count):
+                nc.vector.tensor_tensor(
+                    out=e_rows[k, c][:, j, :],
+                    in0=e_rows[k, c][:, j, :],
+                    in1=grad_banks[k, c, j][:],
+                    op=ALU.mult,
+                )
+            if count < PACK:
+                nc.gpsimd.tensor_tensor(
+                    out=e_rows[k, c][:, count:, :],
+                    in0=e_rows[k, c][:, count:, :],
+                    in1=grad_rows[k, c][:, count:, :],
+                    op=ALU.mult,
+                )
+
         def regroup_e(k, c):
             if c == 0:
                 grouped = grouped_pool.tile([P, PASSES, WIDTH, PACK], BF16, align_bytes=64)
                 e_grouped[k] = grouped
-            copy = nc.scalar.copy if c == 0 else nc.vector.tensor_copy
+            on_scalar = c == 0 and k not in VECTOR_REGROUPS
+            copy = nc.scalar.copy if on_scalar else nc.vector.tensor_copy
             regroup(copy, e_grouped[k][:, c, :, :], e_rows[k, c][:])
 
         def quantise_e(k):
@@ -173,7 +229,7 @@ def tile_dynamic_estimator_v_kernel(tc, x, mean, rho, quad, grad_out, out):
 
         def column_sums(k, t):
             if t == 0:
-                bank = s0_pool.tile([P, CHUNK_TILES, P], F32)
+                bank = s0_pool.tile([P, CHUNK_TILES, SUM_COLUMNS], F32)
                 s0_bank[k] = bank
             slices = [(c, j) for c in range(PASSES) for j in range(PACK)]
             for c, j in slices:
@@ -264,7 +320,20 @@ def tile_dynamic_estimator_v_kernel(tc, x, mean, rho, quad, grad_out, out):
 
         def times_mean(i):
             a_tile = a_pool.tile([P, FEATURES], F32)
-            nc.gpsimd.tensor_tensor(out=a_tile[:], in0=q_tiles[i][:], in1=mean_tile(i), op=ALU.mult)
+            width = WIDTH if i == CLASS_TILES - 1 else FEATURES
+            nc.gpsimd.tensor_tensor(
+                out=a_tile[:, :width],
+                in0=q_tiles[i][:, :width],
+                in1=mean_tile(i)[:, :width],
+                op=ALU.mult,
+            )
+            if width < FEATURES:
+                nc.vector.tensor_tensor(
+                    out=a_tile[:, width:],
+                    in0=q_tiles[i][:, width:],
+                    in1=mean_tile(i)[:, width:],
+                    op=ALU.mult,
+                )
             a_tiles[i] = a_tile
 
         def plus_half_p2(i):
@@ -315,41 +384,44 @@ def tile_dynamic_estimator_v_kernel(tc, x, mean, rho, quad, grad_out, out):
         load_x(0, 0)
         load_x(1, 0)
         load_e(0, 0)
-        load_e(0, 1)
+        load_quad(0, 1)
         load_x(0, 1)
+        load_grad(0, 1)
         load_x(1, 1)
         rho_rows[0] = load_class_rows(rho_pool, rho, 0)
-        rho_rows[1] = load_class_rows(rho_pool, rho, 1)
         load_e(1, 0)
+        rho_rows[1] = load_class_rows(rho_pool, rho, 1)
         mean_rows[0] = load_class_rows(mean_pool, mean, 0)
         load_e(1, 1)
 
         square_x_on_scalar(0, 0)
         regroup_x(0, 0)
-        regroup_x(1, 0)
         quantise_x(0, 0)
-        square_x(1, 0)
-        quantise_square(0, 0)
+        regroup_x(1, 0)
         quantise_x(1, 0)
+        quantise_square(0, 0)
+        exponential(0, 0)
+        multiply(0, 0)
+        square_x_on_scalar(1, 0)
         quantise_square(1, 0)
-        for c in range(PASSES):
-            exponential(0, c)
-            multiply(0, c)
+        regroup_x(0, 1)
+        exponential(0, 1)
+        multiply(0, 1)
         regroup_e(0, 0)
         for t in range(CHUNK_TILES):
             column_sums(0, t)
-        regroup_x(0, 1)
         regroup_e(0, 1)
-        square_x(0, 1)
         regroup_x(1, 1)
         quantise_x(0, 1)
         quantise_e(0)
-        square_x(1, 1)
-        quantise_square(0, 1)
         quantise_x(1, 1)
         copy_sums(0, 0)
+        square_x(0, 1)
+        square_x(1, 1)
+        quantise_square(0, 1)
         quantise_square(1, 1)
         first_moment(0)
+        copy_grad(1, 0, PACK)
         first_moment(1)
         for i in range(0, 4):
             tanh_rho(i)
@@ -363,33 +435,39 @@ def tile_dynamic_estimator_v_kernel(tc, x, mean, rho, quad, grad_out, out):
 
         last = CLASS_TILES - 1
         for s in range(-2, CLASS_TILES):
-            if s == -2:
-                multiply(1, 0)
-                regroup_e(1, 0)
             if s >= 0:
                 plus_half_p2(s)
+            if s == -1:
+                multiply_from_psum(1, 0, PACK)
+                regroup_e(1, 0)
             if s + 2 <= last:
                 mean_s0_minus_p1(s + 2)
             if 0 <= s + 1 <= last:
                 times_mean(s + 1)
 
+            following, phase = divmod(s + 6, CHUNK_TILES)
+            make_e = 1 <= following < CHUNKS and s >= 0
+            if make_e and phase == 1:
+                multiply_from_psum(following, 1, VECTOR_ROWS)
+            if make_e and phase == 2:
+                if following == 1:
+                    multiply_from_psum(1, 1, VECTOR_ROWS)
+                if following in VECTOR_REGROUPS:
+                    regroup_e(following, 0)
+
             late_results = 7 <= s <= 10
             if 0 <= s < FIRST_SPLIT_TILE and not late_results:
                 times_one_plus_tanh(s)
-
-            following, phase = divmod(s + 6, CHUNK_TILES)
-            if 1 <= following < CHUNKS and s >= -1:
-                if phase == 0:
-                    multiply(following, 0)
+            if make_e and phase == 0:
+                multiply_from_psum(following, 0, VECTOR_ROWS)
+                if following not in VECTOR_REGROUPS:
                     regroup_e(following, 0)
-                if phase == 1:
-                    multiply(following, 1)
-                if phase == 2:
-                    regroup_e(following, 1)
-                if phase == 3:
-                    quantise_e(following)
+            if make_e and phase == 2:
+                regroup_e(following, 1)
+            if make_e and phase == 3:
+                quantise_e(following)
 
-            if s == -2:
+            if s == -1:
                 for c in range(PASSES):
                     exponential(2, c)
             if s in (-1, 0, 2, 3):
@@ -440,8 +518,15 @@ def tile_dynamic_estimator_v_kernel(tc, x, mean, rho, quad, grad_out, out):
                 second_moment(s + 1)
             if 2 <= s + 3 <= last:
                 first_moment(s + 3)
+            next_chunk, next_phase = divmod(s + 7, CHUNK_TILES)
+            if s == -1:
+                copy_grad(1, 1, VECTOR_ROWS)
+            elif 2 <= next_chunk < CHUNKS and next_phase < PASSES:
+                copy_grad(next_chunk, next_phase, VECTOR_ROWS)
             sums_chunk, sums_tile = divmod(s + 5, CHUNK_TILES)
-            if 1 <= sums_chunk < CHUNKS:
+            if s == 0:
+                column_sums(1, 0)
+            if 1 <= sums_chunk < CHUNKS and s >= 0:
                 column_sums(sums_chunk, sums_tile)
         for i in range(ROUND_TILES, CLASS_TILES):
             finish(i)

@@ -27,7 +27,6 @@ LEAD_PAIRS = 1
 CLASS_TILES = CLASSES // P
 WORK_SLOTS = 8
 SUM_COLUMNS = 64
-VECTOR_REGROUPS = (3,)
 VECTOR_ROWS = 3
 FIRST_SPLIT_TILE = 11
 
@@ -213,8 +212,7 @@ def tile_dynamic_estimator_v_kernel(tc, x, mean, rho, quad, grad_out, out):
             if c == 0:
                 grouped = grouped_pool.tile([P, PASSES, WIDTH, PACK], BF16, align_bytes=64)
                 e_grouped[k] = grouped
-            on_scalar = c == 0 and k not in VECTOR_REGROUPS
-            copy = nc.scalar.copy if on_scalar else nc.vector.tensor_copy
+            copy = nc.scalar.copy if c == 0 else nc.vector.tensor_copy
             regroup(copy, e_grouped[k][:, c, :, :], e_rows[k, c][:])
 
         def quantise_e(k):
@@ -408,21 +406,23 @@ def tile_dynamic_estimator_v_kernel(tc, x, mean, rho, quad, grad_out, out):
         exponential(0, 1)
         multiply(0, 1)
         regroup_e(0, 0)
-        for t in range(CHUNK_TILES):
-            column_sums(0, t)
+        column_sums(0, 0)
+        column_sums(0, 1)
         regroup_e(0, 1)
         regroup_x(1, 1)
         quantise_x(0, 1)
         quantise_e(0)
         quantise_x(1, 1)
-        copy_sums(0, 0)
         square_x(0, 1)
         square_x(1, 1)
         quantise_square(0, 1)
         quantise_square(1, 1)
+        copy_sums(0, 0)
         first_moment(0)
         copy_grad(1, 0, PACK)
         first_moment(1)
+        column_sums(0, 2)
+        column_sums(0, 3)
         for i in range(0, 4):
             tanh_rho(i)
         exponential(1, 0)
@@ -452,16 +452,13 @@ def tile_dynamic_estimator_v_kernel(tc, x, mean, rho, quad, grad_out, out):
             if make_e and phase == 2:
                 if following == 1:
                     multiply_from_psum(1, 1, VECTOR_ROWS)
-                if following in VECTOR_REGROUPS:
-                    regroup_e(following, 0)
 
             late_results = 7 <= s <= 10
             if 0 <= s < FIRST_SPLIT_TILE and not late_results:
                 times_one_plus_tanh(s)
             if make_e and phase == 0:
-                multiply_from_psum(following, 0, VECTOR_ROWS)
-                if following not in VECTOR_REGROUPS:
-                    regroup_e(following, 0)
+                multiply(following, 0)
+                regroup_e(following, 0)
             if make_e and phase == 2:
                 regroup_e(following, 1)
             if make_e and phase == 3:
@@ -518,11 +515,8 @@ def tile_dynamic_estimator_v_kernel(tc, x, mean, rho, quad, grad_out, out):
                 second_moment(s + 1)
             if 2 <= s + 3 <= last:
                 first_moment(s + 3)
-            next_chunk, next_phase = divmod(s + 7, CHUNK_TILES)
-            if s == -1:
-                copy_grad(1, 1, VECTOR_ROWS)
-            elif 2 <= next_chunk < CHUNKS and next_phase < PASSES:
-                copy_grad(next_chunk, next_phase, VECTOR_ROWS)
+            if s in (-1, 2, 6):
+                copy_grad((s + 6) // CHUNK_TILES, 1, VECTOR_ROWS)
             sums_chunk, sums_tile = divmod(s + 5, CHUNK_TILES)
             if s == 0:
                 column_sums(1, 0)

@@ -225,26 +225,35 @@ def tile_dynamic_estimator_v_kernel(tc, x, mean, rho, quad, grad_out, out):
                 in_=e_grouped[k][:].rearrange("p c w j -> p (c w j)"),
             )
 
-        def column_sums(k, t):
-            if t == 0:
-                bank = s0_pool.tile([P, CHUNK_TILES, SUM_COLUMNS], F32)
-                s0_bank[k] = bank
-            slices = [(c, j) for c in range(PASSES) for j in range(PACK)]
-            for c, j in slices:
-                nc.tensor.matmul(
-                    out=s0_bank[k][:, t, :],
-                    lhsT=e_rows[k, c][:, j, t * P : (t + 1) * P],
-                    rhs=halves[:],
-                    start=((c, j) == slices[0]),
-                    stop=((c, j) == slices[-1]),
-                )
+        def column_sums(k, t, passes=range(PASSES)):
+            for c in passes:
+                for j in range(PACK):
+                    nc.tensor.matmul(
+                        out=s0_bank[k, t],
+                        lhsT=e_rows[k, c][:, j, t * P : (t + 1) * P],
+                        rhs=halves[:],
+                        start=(c == 0 and j == 0),
+                        stop=(c == PASSES - 1 and j == PACK - 1),
+                    )
 
-        def copy_sums(k, a):
-            if a == 0:
-                sums = sums_pool.tile([P, CHUNK_TILES, 1], F32)
+        def sums_in_one_bank(k):
+            bank = s0_pool.tile([P, CHUNK_TILES, SUM_COLUMNS], F32)
+            for t in range(CHUNK_TILES):
+                s0_bank[k, t] = bank[:, t, :]
+
+        def sums_in_four_banks(k):
+            bank = s0_pool.tile([P, CHUNK_TILES, SUM_COLUMNS], F32)
+            s0_bank[k, 0] = bank[:, 0, :]
+            for t in range(1, CHUNK_TILES):
+                g_bank = g_pool.tile([P, SUM_COLUMNS], F32)
+                s0_bank[k, t] = g_bank[:]
+
+        def copy_sums(k, tiles):
+            if 0 in tiles:
+                sums = sums_pool.tile([P, CHUNK_TILES], F32)
                 half_s0[k] = sums
-            pair = slice(2 * a, 2 * a + 2)
-            nc.vector.tensor_copy(out=half_s0[k][:, pair, :], in_=s0_bank[k][:, pair, 0:1])
+            for t in tiles:
+                nc.vector.tensor_copy(out=half_s0[k][:, t : t + 1], in_=s0_bank[k, t][:, 0:1])
 
         def tanh_rho(i):
             k, t = divmod(i, CHUNK_TILES)
@@ -309,7 +318,7 @@ def tile_dynamic_estimator_v_kernel(tc, x, mean, rho, quad, grad_out, out):
                 nc.vector.scalar_tensor_tensor(
                     out=q_tile[:, piece(h)],
                     in0=mean_tile(i)[:, piece(h)],
-                    scalar=half_s0[k][:, t, :],
+                    scalar=half_s0[k][:, t : t + 1],
                     in1=p1[i, h][:],
                     op0=ALU.mult,
                     op1=ALU.subtract,
@@ -400,14 +409,17 @@ def tile_dynamic_estimator_v_kernel(tc, x, mean, rho, quad, grad_out, out):
         quantise_square(0, 0)
         exponential(0, 0)
         multiply(0, 0)
+        sums_in_four_banks(0)
+        for t in range(CHUNK_TILES):
+            column_sums(0, t, (0,))
         square_x_on_scalar(1, 0)
         quantise_square(1, 0)
         regroup_x(0, 1)
         exponential(0, 1)
         multiply(0, 1)
+        for t in range(CHUNK_TILES):
+            column_sums(0, t, (1,))
         regroup_e(0, 0)
-        column_sums(0, 0)
-        column_sums(0, 1)
         regroup_e(0, 1)
         regroup_x(1, 1)
         quantise_x(0, 1)
@@ -417,12 +429,10 @@ def tile_dynamic_estimator_v_kernel(tc, x, mean, rho, quad, grad_out, out):
         square_x(1, 1)
         quantise_square(0, 1)
         quantise_square(1, 1)
-        copy_sums(0, 0)
+        copy_sums(0, range(CHUNK_TILES))
         first_moment(0)
         copy_grad(1, 0, PACK)
         first_moment(1)
-        column_sums(0, 2)
-        column_sums(0, 3)
         for i in range(0, 4):
             tanh_rho(i)
         exponential(1, 0)
@@ -507,9 +517,9 @@ def tile_dynamic_estimator_v_kernel(tc, x, mean, rho, quad, grad_out, out):
                 times_one_plus_tanh(s)
 
             if (s + 3) % CHUNK_TILES == 0 and 1 <= (s + 3) // CHUNK_TILES < CHUNKS:
-                copy_sums((s + 3) // CHUNK_TILES, 0)
-            if (s + 1) % CHUNK_TILES == 0 and (s + 1) // CHUNK_TILES < CHUNKS:
-                copy_sums((s + 1) // CHUNK_TILES, 1)
+                copy_sums((s + 3) // CHUNK_TILES, (0, 1))
+            if (s + 1) % CHUNK_TILES == 0 and 1 <= (s + 1) // CHUNK_TILES < CHUNKS:
+                copy_sums((s + 1) // CHUNK_TILES, (2, 3))
 
             if 0 <= s + 1 <= last:
                 second_moment(s + 1)
@@ -519,8 +529,11 @@ def tile_dynamic_estimator_v_kernel(tc, x, mean, rho, quad, grad_out, out):
                 copy_grad((s + 6) // CHUNK_TILES, 1, VECTOR_ROWS)
             sums_chunk, sums_tile = divmod(s + 5, CHUNK_TILES)
             if s == 0:
+                sums_in_one_bank(1)
                 column_sums(1, 0)
             if 1 <= sums_chunk < CHUNKS and s >= 0:
+                if sums_tile == 0:
+                    sums_in_one_bank(sums_chunk)
                 column_sums(sums_chunk, sums_tile)
         for i in range(ROUND_TILES, CLASS_TILES):
             finish(i)

@@ -26,7 +26,7 @@ ROUND_TILES = 2 * CHUNK_TILES
 LEAD_PAIRS = 1
 CLASS_TILES = CLASSES // P
 WORK_SLOTS = 8
-SUM_COLUMNS = 64
+SUM_COLUMNS = 128
 VECTOR_ROWS = 3
 FIRST_SPLIT_TILE = 11
 

@@ -124,10 +124,12 @@ def tile_dynamic_estimator_v_kernel(tc, x, mean, rho, quad, grad_out, out):
 
         def load_class_rows(pool, source, k):
             class_rows = pool.tile([P, CHUNK_TILES, FEATURES], BF16)
-            nc.sync.dma_start(
-                out=class_rows[:], in_=source[piece(k), :].rearrange("(t p) d -> p t d", p=P)
-            )
+            load_class_tiles(class_rows, source, k, slice(0, CHUNK_TILES))
             return class_rows
+
+        def load_class_tiles(class_rows, source, k, tiles):
+            chunk_rows = source[piece(k), :].rearrange("(t p) d -> p t d", p=P)
+            nc.sync.dma_start(out=class_rows[:, tiles, :], in_=chunk_rows[:, tiles, :])
 
         def regroup(copy, grouped, rows):
             copy(
@@ -388,18 +390,30 @@ def tile_dynamic_estimator_v_kernel(tc, x, mean, rho, quad, grad_out, out):
             )
             nc.sync.dma_start(out=out[i * P : (i + 1) * P, :], in_=y_tiles[i][:])
 
+        first, second = slice(0, 2), slice(2, 4)
+        for k in range(2):
+            class_rows = rho_pool.tile([P, CHUNK_TILES, FEATURES], BF16)
+            rho_rows[k] = class_rows
+        class_rows = mean_pool.tile([P, CHUNK_TILES, FEATURES], BF16)
+        mean_rows[0] = class_rows
         load_x(0, 0)
         load_x(1, 0)
-        load_e(0, 0)
+        load_quad(0, 0)
+        load_grad(0, 0)
         load_quad(0, 1)
         load_x(0, 1)
         load_grad(0, 1)
+        load_class_tiles(rho_rows[0], rho, 0, first)
         load_x(1, 1)
-        rho_rows[0] = load_class_rows(rho_pool, rho, 0)
-        load_e(1, 0)
-        rho_rows[1] = load_class_rows(rho_pool, rho, 1)
-        mean_rows[0] = load_class_rows(mean_pool, mean, 0)
-        load_e(1, 1)
+        load_class_tiles(rho_rows[0], rho, 0, second)
+        load_quad(1, 0)
+        load_class_tiles(rho_rows[1], rho, 1, first)
+        load_class_tiles(mean_rows[0], mean, 0, first)
+        load_grad(1, 0)
+        load_class_tiles(rho_rows[1], rho, 1, second)
+        load_quad(1, 1)
+        load_class_tiles(mean_rows[0], mean, 0, second)
+        load_grad(1, 1)
 
         square_x_on_scalar(0, 0)
         regroup_x(0, 0)
@@ -439,9 +453,11 @@ def tile_dynamic_estimator_v_kernel(tc, x, mean, rho, quad, grad_out, out):
         for i in range(4, 8):
             tanh_rho(i)
         exponential(1, 1)
-        for c in range(PASSES):
-            load_e(2, c)
+        load_quad(2, 0)
+        load_quad(2, 1)
+        load_grad(2, 0)
         mean_rows[1] = load_class_rows(mean_pool, mean, 1)
+        load_grad(2, 1)
 
         last = CLASS_TILES - 1
         for s in range(-2, CLASS_TILES):
@@ -485,7 +501,9 @@ def tile_dynamic_estimator_v_kernel(tc, x, mean, rho, quad, grad_out, out):
                 rho_rows[3] = load_class_rows(rho_pool, rho, 3)
             if s == 4:
                 for c in range(PASSES):
-                    load_e(3, c)
+                    load_quad(3, c)
+                for c in range(PASSES):
+                    load_grad(3, c)
                 mean_rows[2] = load_class_rows(mean_pool, mean, 2)
                 for c in range(PASSES):
                     exponential(3, c)

@@ -51,8 +51,8 @@ def tile_dynamic_estimator_v_kernel(tc, x, mean, rho, quad, grad_out, out):
         codes_pool = sbuf_pool("codes", 2)
         rho_pool = sbuf_pool("rho", 2)
         mean_pool = sbuf_pool("mean", 2)
-        tanh_pool = sbuf_pool("tanh", ROUND_TILES)
-        chain_pool = sbuf_pool("chain", ROUND_TILES)
+        tanh_pool = sbuf_pool("tanh", ROUND_TILES // 2)
+        chain_pool = sbuf_pool("chain", ROUND_TILES // 2)
         q_pool = sbuf_pool("q", 2)
         a_pool = sbuf_pool("a", 2)
         b_pool = sbuf_pool("b", 2)
@@ -84,8 +84,9 @@ def tile_dynamic_estimator_v_kernel(tc, x, mean, rho, quad, grad_out, out):
 
         x_rows, x_grouped, squared = {}, {}, {}
         e_rows, grad_rows, grad_banks, e_grouped = {}, {}, {}, {}
-        e_codes, e_scales, half_s0, s0_bank = {}, {}, {}, {}
+        e_codes, e_scales, half_s0, s0_bank, sums_bank = {}, {}, {}, {}, {}
         rho_rows, mean_rows, tanh_half, chain = {}, {}, {}, {}
+        tanh_pairs, chain_pairs = {}, {}
         p1, p2, q_tiles, a_tiles, v_halves, y_tiles = {}, {}, {}, {}, {}, {}
 
         def piece(index):
@@ -101,10 +102,16 @@ def tile_dynamic_estimator_v_kernel(tc, x, mean, rho, quad, grad_out, out):
         def exp_parts(k):
             return (slice(0, 2), slice(2, 4)) if k == 0 else (slice(0, 4),)
 
-        def load_x(c, h):
-            rows = work_pool.tile([P, PACK, WIDTH], BF16, tag="work", align_bytes=64)
-            nc.sync.dma_start(out=rows[:], in_=batch_rows(x, c, piece(h)))
-            x_rows[c, h] = rows
+        def load_x_half(c, h):
+            chain_pair = chain_pool.tile([P, PACK, WIDTH], BF16)
+            nc.sync.dma_start(out=chain_pair[:], in_=batch_rows(x, c, piece(h)))
+            x_rows[c, h] = chain_pair[:]
+
+        def load_x(c):
+            chain_pair = chain_pool.tile([P, PACK, FEATURES], BF16)
+            nc.sync.dma_start(out=chain_pair[:], in_=batch_rows(x, c, slice(0, FEATURES)))
+            for h in range(FEATURE_HALVES):
+                x_rows[c, h] = chain_pair[:, :, piece(h)]
 
         def load_quad(k, c):
             quad_rows = quad_pool.tile([P, PACK, WIDTH], F32)
@@ -117,10 +124,6 @@ def tile_dynamic_estimator_v_kernel(tc, x, mean, rho, quad, grad_out, out):
             rows = grad_pool.tile([P, PACK, WIDTH], BF16)
             nc.sync.dma_start(out=rows[:], in_=batch_rows(grad_out, c, piece(k)))
             grad_rows[k, c] = rows
-
-        def load_e(k, c):
-            load_quad(k, c)
-            load_grad(k, c)
 
         def load_class_rows(pool, source, k):
             class_rows = pool.tile([P, CHUNK_TILES, FEATURES], BF16)
@@ -140,7 +143,7 @@ def tile_dynamic_estimator_v_kernel(tc, x, mean, rho, quad, grad_out, out):
         def regroup_x(c, h):
             grouped = work_pool.tile([P, WIDTH, PACK], BF16, tag="work", align_bytes=64)
             x_grouped[c, h] = grouped
-            regroup(nc.vector.tensor_copy, grouped[:], x_rows[c, h][:])
+            regroup(nc.vector.tensor_copy, grouped[:], x_rows[c, h])
 
         def square_x(c, h):
             product_tile = work_pool.tile([P, WIDTH, PACK], BF16, tag="work", align_bytes=64)
@@ -154,7 +157,7 @@ def tile_dynamic_estimator_v_kernel(tc, x, mean, rho, quad, grad_out, out):
             squared[c, h] = product_tile
             nc.scalar.activation(
                 out=product_tile[:].rearrange("p (w i) j -> p w j i", i=RUN),
-                in_=x_rows[c, h][:].rearrange("p j (w i) -> p w j i", i=RUN),
+                in_=x_rows[c, h].rearrange("p j (w i) -> p w j i", i=RUN),
                 func=ACT.Square,
             )
 
@@ -240,6 +243,7 @@ def tile_dynamic_estimator_v_kernel(tc, x, mean, rho, quad, grad_out, out):
 
         def sums_in_one_bank(k):
             bank = s0_pool.tile([P, CHUNK_TILES, SUM_COLUMNS], F32)
+            sums_bank[k] = bank
             for t in range(CHUNK_TILES):
                 s0_bank[k, t] = bank[:, t, :]
 
@@ -250,38 +254,52 @@ def tile_dynamic_estimator_v_kernel(tc, x, mean, rho, quad, grad_out, out):
                 g_bank = g_pool.tile([P, SUM_COLUMNS], F32)
                 s0_bank[k, t] = g_bank[:]
 
-        def copy_sums(k, tiles):
-            if 0 in tiles:
-                sums = sums_pool.tile([P, CHUNK_TILES], F32)
+        def copy_sums(k):
+            sums = sums_pool.tile([P, CHUNK_TILES, 1], F32)
+            half_s0[k] = sums
+            for t in range(CHUNK_TILES):
+                nc.vector.tensor_copy(out=half_s0[k][:, t, :], in_=s0_bank[k, t][:, 0:1])
+
+        def copy_sums_of_pair(k, a):
+            if a == 0:
+                sums = sums_pool.tile([P, CHUNK_TILES, 1], F32)
                 half_s0[k] = sums
-            for t in tiles:
-                nc.vector.tensor_copy(out=half_s0[k][:, t : t + 1], in_=s0_bank[k, t][:, 0:1])
-
-        def tanh_rho(i):
-            k, t = divmod(i, CHUNK_TILES)
-            tanh_tile = tanh_pool.tile([P, FEATURES], F32)
-            nc.scalar.activation(
-                out=tanh_tile[:], in_=rho_rows[k][:, t, :], func=ACT.Tanh, scale=0.5
+            pair = slice(2 * a, 2 * a + 2)
+            nc.vector.tensor_copy(
+                out=half_s0[k][:, pair, :], in_=sums_bank[k][:, pair, 0:1]
             )
-            tanh_half[i] = tanh_tile
 
-        def logarithms(pair):
-            for i in pair:
-                chain_tile = chain_pool.tile([P, FEATURES], F32)
+        def both(pair_tile):
+            return pair_tile[:].rearrange("p t d -> p (t d)")
+
+        def tanh_rho(b):
+            k, t = divmod(2 * b, CHUNK_TILES)
+            tanh_pair = tanh_pool.tile([P, 2, FEATURES], F32)
+            nc.scalar.activation(
+                out=tanh_pair[:], in_=rho_rows[k][:, t : t + 2, :], func=ACT.Tanh, scale=0.5
+            )
+            tanh_half[2 * b], tanh_half[2 * b + 1] = tanh_pair[:, 0, :], tanh_pair[:, 1, :]
+            tanh_pairs[b] = tanh_pair
+
+        def logarithms(pairs):
+            for b in pairs:
+                chain_pair = chain_pool.tile([P, 2, FEATURES], F32)
                 nc.scalar.activation(
-                    out=chain_tile[:],
-                    in_=tanh_half[i][:],
+                    out=both(chain_pair),
+                    in_=both(tanh_pairs[b]),
                     func=ACT.Ln,
                     scale=-0.5,
                     bias=halves[:, 0:1],
                 )
-                chain[i] = chain_tile
-            for i in pair:
-                nc.scalar.activation(out=chain[i][:], in_=chain[i][:], func=ACT.Ln, scale=-1.0)
+                chain_pairs[b] = chain_pair
+                chain[2 * b], chain[2 * b + 1] = chain_pair[:, 0, :], chain_pair[:, 1, :]
+            for b in pairs:
+                nc.scalar.activation(
+                    out=both(chain_pairs[b]), in_=both(chain_pairs[b]), func=ACT.Ln, scale=-1.0
+                )
 
-        def inverse_cubes(pair):
-            for i in pair:
-                nc.scalar.activation(out=chain[i][:], in_=chain[i][:], func=ACT.Exp, scale=-3.0)
+        def inverse_cubes(part):
+            nc.scalar.activation(out=part, in_=part, func=ACT.Exp, scale=-3.0)
 
         def product(bank, i, codes, scales, h):
             k, t = divmod(i, CHUNK_TILES)
@@ -320,7 +338,7 @@ def tile_dynamic_estimator_v_kernel(tc, x, mean, rho, quad, grad_out, out):
                 nc.vector.scalar_tensor_tensor(
                     out=q_tile[:, piece(h)],
                     in0=mean_tile(i)[:, piece(h)],
-                    scalar=half_s0[k][:, t : t + 1],
+                    scalar=half_s0[k][:, t, :],
                     in1=p1[i, h][:],
                     op0=ALU.mult,
                     op1=ALU.subtract,
@@ -366,7 +384,7 @@ def tile_dynamic_estimator_v_kernel(tc, x, mean, rho, quad, grad_out, out):
             if i < FIRST_SPLIT_TILE:
                 nc.vector.scalar_tensor_tensor(
                     out=y_tile[:],
-                    in0=tanh_half[i][:],
+                    in0=tanh_half[i],
                     scalar=1.0,
                     in1=a_tiles[i][:],
                     op0=ALU.add,
@@ -386,7 +404,7 @@ def tile_dynamic_estimator_v_kernel(tc, x, mean, rho, quad, grad_out, out):
 
         def finish(i):
             nc.vector.tensor_tensor(
-                out=y_tiles[i][:], in0=y_tiles[i][:], in1=chain[i][:], op=ALU.mult
+                out=y_tiles[i][:], in0=y_tiles[i][:], in1=chain[i], op=ALU.mult
             )
             nc.sync.dma_start(out=out[i * P : (i + 1) * P, :], in_=y_tiles[i][:])
 
@@ -396,15 +414,14 @@ def tile_dynamic_estimator_v_kernel(tc, x, mean, rho, quad, grad_out, out):
             rho_rows[k] = class_rows
         class_rows = mean_pool.tile([P, CHUNK_TILES, FEATURES], BF16)
         mean_rows[0] = class_rows
-        load_x(0, 0)
-        load_x(1, 0)
+        load_x_half(0, 0)
+        load_x(1)
         load_quad(0, 0)
         load_grad(0, 0)
         load_quad(0, 1)
-        load_x(0, 1)
+        load_x_half(0, 1)
         load_grad(0, 1)
         load_class_tiles(rho_rows[0], rho, 0, first)
-        load_x(1, 1)
         load_class_tiles(rho_rows[0], rho, 0, second)
         load_quad(1, 0)
         load_class_tiles(rho_rows[1], rho, 1, first)
@@ -414,6 +431,11 @@ def tile_dynamic_estimator_v_kernel(tc, x, mean, rho, quad, grad_out, out):
         load_quad(1, 1)
         load_class_tiles(mean_rows[0], mean, 0, second)
         load_grad(1, 1)
+        load_quad(2, 0)
+        load_quad(2, 1)
+        load_grad(2, 0)
+        mean_rows[1] = load_class_rows(mean_pool, mean, 1)
+        load_grad(2, 1)
 
         square_x_on_scalar(0, 0)
         regroup_x(0, 0)
@@ -422,42 +444,37 @@ def tile_dynamic_estimator_v_kernel(tc, x, mean, rho, quad, grad_out, out):
         quantise_x(1, 0)
         quantise_square(0, 0)
         exponential(0, 0)
+        regroup_x(1, 1)
         multiply(0, 0)
         sums_in_four_banks(0)
         for t in range(CHUNK_TILES):
             column_sums(0, t, (0,))
         square_x_on_scalar(1, 0)
+        quantise_x(1, 1)
         quantise_square(1, 0)
-        regroup_x(0, 1)
         exponential(0, 1)
+        regroup_x(0, 1)
         multiply(0, 1)
         for t in range(CHUNK_TILES):
             column_sums(0, t, (1,))
         regroup_e(0, 0)
         regroup_e(0, 1)
-        regroup_x(1, 1)
         quantise_x(0, 1)
         quantise_e(0)
-        quantise_x(1, 1)
         square_x(0, 1)
         square_x(1, 1)
         quantise_square(0, 1)
         quantise_square(1, 1)
-        copy_sums(0, range(CHUNK_TILES))
+        copy_sums(0)
         first_moment(0)
         copy_grad(1, 0, PACK)
         first_moment(1)
-        for i in range(0, 4):
-            tanh_rho(i)
+        tanh_rho(0)
+        tanh_rho(1)
         exponential(1, 0)
-        for i in range(4, 8):
-            tanh_rho(i)
+        tanh_rho(2)
+        tanh_rho(3)
         exponential(1, 1)
-        load_quad(2, 0)
-        load_quad(2, 1)
-        load_grad(2, 0)
-        mean_rows[1] = load_class_rows(mean_pool, mean, 1)
-        load_grad(2, 1)
 
         last = CLASS_TILES - 1
         for s in range(-2, CLASS_TILES):
@@ -493,9 +510,8 @@ def tile_dynamic_estimator_v_kernel(tc, x, mean, rho, quad, grad_out, out):
             if s == -1:
                 for c in range(PASSES):
                     exponential(2, c)
-            if s in (-1, 0, 2, 3):
-                first = 2 * (s + 1) if s < 2 else 2 * s
-                logarithms((first, first + 1))
+            if s in (-1, 2):
+                logarithms((0, 1) if s < 0 else (2, 3))
             if s == 2:
                 rho_rows[2] = load_class_rows(rho_pool, rho, 2)
                 rho_rows[3] = load_class_rows(rho_pool, rho, 3)
@@ -507,25 +523,24 @@ def tile_dynamic_estimator_v_kernel(tc, x, mean, rho, quad, grad_out, out):
                 mean_rows[2] = load_class_rows(mean_pool, mean, 2)
                 for c in range(PASSES):
                     exponential(3, c)
-                inverse_cubes((0, 1))
+                inverse_cubes(both(chain_pairs[0]))
             if s == 5:
-                inverse_cubes((2, 3))
-                tanh_rho(8)
-                tanh_rho(9)
+                inverse_cubes(both(chain_pairs[1]))
+                tanh_rho(4)
             if s == 6:
-                tanh_rho(10)
-                tanh_rho(11)
-                inverse_cubes((4, 5))
+                tanh_rho(5)
+                inverse_cubes(both(chain_pairs[2]))
             if s == 7:
-                inverse_cubes((6, 7))
-                for i in range(12, 16):
-                    tanh_rho(i)
+                inverse_cubes(both(chain_pairs[3]))
+                tanh_rho(6)
+                tanh_rho(7)
             if s == 8:
                 mean_rows[3] = load_class_rows(mean_pool, mean, 3)
-            if 8 <= s <= 11:
-                logarithms((2 * s - 8, 2 * s - 7))
+            if s in (8, 10):
+                logarithms((4, 5) if s == 8 else (6, 7))
             if 12 <= s <= 15:
-                inverse_cubes((2 * s - 16, 2 * s - 15))
+                inverse_cubes(chain[2 * s - 16])
+                inverse_cubes(chain[2 * s - 15])
 
             if late_results:
                 finish(2 * s - 14)
@@ -535,9 +550,9 @@ def tile_dynamic_estimator_v_kernel(tc, x, mean, rho, quad, grad_out, out):
                 times_one_plus_tanh(s)
 
             if (s + 3) % CHUNK_TILES == 0 and 1 <= (s + 3) // CHUNK_TILES < CHUNKS:
-                copy_sums((s + 3) // CHUNK_TILES, (0, 1))
+                copy_sums_of_pair((s + 3) // CHUNK_TILES, 0)
             if (s + 1) % CHUNK_TILES == 0 and 1 <= (s + 1) // CHUNK_TILES < CHUNKS:
-                copy_sums((s + 1) // CHUNK_TILES, (2, 3))
+                copy_sums_of_pair((s + 1) // CHUNK_TILES, 1)
 
             if 0 <= s + 1 <= last:
                 second_moment(s + 1)

from contextlib import ExitStack

import concourse.mybir as mybir
from concourse.masks import make_identity

F32 = mybir.dt.float32
BF16 = mybir.dt.bfloat16
U32 = mybir.dt.uint32
U8 = mybir.dt.uint8
E4M3_X4 = mybir.dt.float8_e4m3fn_x4
E5M2_X4 = mybir.dt.float8_e5m2_x4
ACT = mybir.ActivationFunctionType
ALU = mybir.AluOpType

BATCH, CLASSES, FEATURES = 1024, 2048, 1024
P = 128
PACK = 4
K_PASS = P * PACK
PASSES = BATCH // K_PASS
WIDTH = 512
CHUNKS = CLASSES // WIDTH
CHUNK_TILES = WIDTH // P
FEATURE_HALVES = FEATURES // WIDTH
RUN = 4
ROUND_TILES = 2 * CHUNK_TILES
LEAD_PAIRS = 1
CLASS_TILES = CLASSES // P
WORK_SLOTS = 8
SUM_COLUMNS = 128
VECTOR_ROWS = 3
FIRST_SPLIT_TILE = 11

FLOPS = 2 * 2 * BATCH * CLASSES * FEATURES


def tile_dynamic_estimator_v_kernel(tc, x, mean, rho, quad, grad_out, out):
    nc = tc.nc
    with ExitStack() as stack:

        def sbuf_pool(name, bufs):
            return stack.enter_context(tc.tile_pool(name=name, bufs=bufs))

        def psum_pool(name, bufs):
            return stack.enter_context(tc.psum_pool(name=name, bufs=bufs))

        keep = sbuf_pool("keep", 1)
        quad_pool = sbuf_pool("quad", 2 * PASSES)
        grad_pool = sbuf_pool("grad", 2 * PASSES)
        grouped_pool = sbuf_pool("grouped", 1)
        work_pool = sbuf_pool("work", WORK_SLOTS)
        codes_pool = sbuf_pool("codes", 2)
        rho_pool = sbuf_pool("rho", 2)
        mean_pool = sbuf_pool("mean", 2)
        tanh_pool = sbuf_pool("tanh", ROUND_TILES // 2)
        chain_pool = sbuf_pool("chain", ROUND_TILES // 2)
        q_pool = sbuf_pool("q", 2)
        a_pool = sbuf_pool("a", 2)
        b_pool = sbuf_pool("b", 2)
        sums_pool = sbuf_pool("sums", 2)
        p1_pool = psum_pool("p1", 2)
        p2_pool = psum_pool("p2", 2)
        g_pool = psum_pool("g", VECTOR_ROWS)
        s0_pool = psum_pool("s0", 1)

        x_codes = keep.tile([P, PASSES, FEATURES], U32, align_bytes=64)
        x_scales = keep.tile([P, PASSES, FEATURES], U8, align_bytes=64)
        xx_codes = keep.tile([P, PASSES, FEATURES], U32, align_bytes=64)
        xx_scales = keep.tile([P, PASSES, FEATURES], U8, align_bytes=64)
        halves = keep.tile([P, SUM_COLUMNS], F32)
        nc.gpsimd.memset(halves[:], 0.5)
        identity = keep.tile([P, P], BF16)
        make_identity(nc, identity[:])

        stack.enter_context(
            tc.manual_schedule(
                engines={
                    mybir.EngineType.Activation,
                    mybir.EngineType.DVE,
                    mybir.EngineType.PE,
                    mybir.EngineType.Pool,
                }
            )
        )

        x_rows, x_grouped, squared = {}, {}, {}
        e_rows, grad_rows, grad_banks, e_grouped = {}, {}, {}, {}
        e_codes, e_scales, half_s0, s0_bank, sums_bank = {}, {}, {}, {}, {}
        rho_rows, mean_rows, tanh_half, chain = {}, {}, {}, {}
        tanh_pairs, chain_pairs = {}, {}
        p1, p2, q_tiles, a_tiles, v_halves, y_tiles = {}, {}, {}, {}, {}, {}

        def piece(index):
            return slice(index * WIDTH, (index + 1) * WIDTH)

        def batch_rows(source, c, cols):
            rows = slice(c * K_PASS, (c + 1) * K_PASS)
            return source[rows, cols].rearrange("(p j) w -> p j w", j=PACK)

        def flat(grouped):
            return grouped[:].rearrange("p w j -> p (w j)")

        def exp_parts(k):
            return (slice(0, 2), slice(2, 4)) if k == 0 else (slice(0, 4),)

        def load_x_half(c, h):
            chain_pair = chain_pool.tile([P, PACK, WIDTH], BF16)
            nc.sync.dma_start(out=chain_pair[:], in_=batch_rows(x, c, piece(h)))
            x_rows[c, h] = chain_pair[:]

        def load_x(c):
            chain_pair = chain_pool.tile([P, PACK, FEATURES], BF16)
            nc.sync.dma_start(out=chain_pair[:], in_=batch_rows(x, c, slice(0, FEATURES)))
            for h in range(FEATURE_HALVES):
                x_rows[c, h] = chain_pair[:, :, piece(h)]

        def load_quad(k, c):
            quad_rows = quad_pool.tile([P, PACK, WIDTH], F32)
            source = batch_rows(quad, c, piece(k))
            for rows in exp_parts(k):
                nc.sync.dma_start(out=quad_rows[:, rows, :], in_=source[:, rows, :])
            e_rows[k, c] = quad_rows

        def load_grad(k, c):
            rows = grad_pool.tile([P, PACK, WIDTH], BF16)
            nc.sync.dma_start(out=rows[:], in_=batch_rows(grad_out, c, piece(k)))
            grad_rows[k, c] = rows

        def load_class_rows(pool, source, k):
            class_rows = pool.tile([P, CHUNK_TILES, FEATURES], BF16)
            load_class_tiles(class_rows, source, k, slice(0, CHUNK_TILES))
            return class_rows

        def load_class_tiles(class_rows, source, k, tiles):
            chunk_rows = source[piece(k), :].rearrange("(t p) d -> p t d", p=P)
            nc.sync.dma_start(out=class_rows[:, tiles, :], in_=chunk_rows[:, tiles, :])

        def regroup(copy, grouped, rows):
            copy(
                out=grouped.rearrange("p (w i) j -> p w j i", i=RUN),
                in_=rows.rearrange("p j (w i) -> p w j i", i=RUN),
            )

        def regroup_x(c, h):
            grouped = work_pool.tile([P, WIDTH, PACK], BF16, tag="work", align_bytes=64)
            x_grouped[c, h] = grouped
            regroup(nc.vector.tensor_copy, grouped[:], x_rows[c, h])

        def square_x(c, h):
            product_tile = work_pool.tile([P, WIDTH, PACK], BF16, tag="work", align_bytes=64)
            squared[c, h] = product_tile
            nc.vector.tensor_tensor(
                out=product_tile[:], in0=x_grouped[c, h][:], in1=x_grouped[c, h][:], op=ALU.mult
            )

        def square_x_on_scalar(c, h):
            product_tile = work_pool.tile([P, WIDTH, PACK], BF16, tag="work", align_bytes=64)
            squared[c, h] = product_tile
            nc.scalar.activation(
                out=product_tile[:].rearrange("p (w i) j -> p w j i", i=RUN),
                in_=x_rows[c, h].rearrange("p j (w i) -> p w j i", i=RUN),
                func=ACT.Square,
            )

        def quantise_x(c, h):
            nc.vector.quantize_mx(
                out=x_codes[:, c, piece(h)].bitcast(E4M3_X4),
                scales=x_scales[:, c, piece(h)],
                in_=flat(x_grouped[c, h]),
            )

        def quantise_square(c, h):
            nc.vector.quantize_mx(
                out=xx_codes[:, c, piece(h)].bitcast(E4M3_X4),
                scales=xx_scales[:, c, piece(h)],
                in_=flat(squared[c, h]),
            )

        def exponential(k, c):
            for rows in exp_parts(k):
                e_part = e_rows[k, c][:, rows, :]
                nc.scalar.activation(out=e_part, in_=e_part, func=ACT.Exp, scale=-1.0)

        def copy_grad(k, c, count):
            for j in range(count):
                g_bank = g_pool.tile([P, WIDTH], F32)
                nc.tensor.matmul(
                    out=g_bank[:],
                    lhsT=identity[:],
                    rhs=grad_rows[k, c][:, j, :],
                    start=True,
                    stop=True,
                )
                grad_banks[k, c, j] = g_bank

        def multiply(k, c):
            nc.vector.tensor_tensor(
                out=e_rows[k, c][:], in0=e_rows[k, c][:], in1=grad_rows[k, c][:], op=ALU.mult
            )

        def multiply_from_psum(k, c, count):
            for j in range(count):
                nc.vector.tensor_tensor(
                    out=e_rows[k, c][:, j, :],
                    in0=e_rows[k, c][:, j, :],
                    in1=grad_banks[k, c, j][:],
                    op=ALU.mult,
                )
            if count < PACK:
                nc.gpsimd.tensor_tensor(
                    out=e_rows[k, c][:, count:, :],
                    in0=e_rows[k, c][:, count:, :],
                    in1=grad_rows[k, c][:, count:, :],
                    op=ALU.mult,
                )

        def regroup_e(k, c):
            if c == 0:
                grouped = grouped_pool.tile([P, PASSES, WIDTH, PACK], BF16, align_bytes=64)
                e_grouped[k] = grouped
            copy = nc.scalar.copy if c == 0 else nc.vector.tensor_copy
            regroup(copy, e_grouped[k][:, c, :, :], e_rows[k, c][:])

        def quantise_e(k):
            codes = codes_pool.tile([P, PASSES, WIDTH], U32, align_bytes=64)
            scales = codes_pool.tile([P, PASSES, WIDTH], U8, align_bytes=64)
            e_codes[k], e_scales[k] = codes, scales
            nc.vector.quantize_mx(
                out=codes[:].rearrange("p c w -> p (c w)").bitcast(E5M2_X4),
                scales=scales[:].rearrange("p c w -> p (c w)"),
                in_=e_grouped[k][:].rearrange("p c w j -> p (c w j)"),
            )

        def column_sums(k, t, passes=range(PASSES)):
            for c in passes:
                for j in range(PACK):
                    nc.tensor.matmul(
                        out=s0_bank[k, t],
                        lhsT=e_rows[k, c][:, j, t * P : (t + 1) * P],
                        rhs=halves[:],
                        start=(c == 0 and j == 0),
                        stop=(c == PASSES - 1 and j == PACK - 1),
                    )

        def sums_in_one_bank(k):
            bank = s0_pool.tile([P, CHUNK_TILES, SUM_COLUMNS], F32)
            sums_bank[k] = bank
            for t in range(CHUNK_TILES):
                s0_bank[k, t] = bank[:, t, :]

        def sums_in_four_banks(k):
            bank = s0_pool.tile([P, CHUNK_TILES, SUM_COLUMNS], F32)
            s0_bank[k, 0] = bank[:, 0, :]
            for t in range(1, CHUNK_TILES):
                g_bank = g_pool.tile([P, SUM_COLUMNS], F32)
                s0_bank[k, t] = g_bank[:]

        def copy_sums(k):
            sums = sums_pool.tile([P, CHUNK_TILES, 1], F32)
            half_s0[k] = sums
            for t in range(CHUNK_TILES):
                nc.vector.tensor_copy(out=half_s0[k][:, t, :], in_=s0_bank[k, t][:, 0:1])

        def copy_sums_of_pair(k, a):
            if a == 0:
                sums = sums_pool.tile([P, CHUNK_TILES, 1], F32)
                half_s0[k] = sums
            pair = slice(2 * a, 2 * a + 2)
            nc.vector.tensor_copy(
                out=half_s0[k][:, pair, :], in_=sums_bank[k][:, pair, 0:1]
            )

        def both(pair_tile):
            return pair_tile[:].rearrange("p t d -> p (t d)")

        def tanh_rho(b):
            k, t = divmod(2 * b, CHUNK_TILES)
            tanh_pair = tanh_pool.tile([P, 2, FEATURES], F32)
            nc.scalar.activation(
                out=tanh_pair[:], in_=rho_rows[k][:, t : t + 2, :], func=ACT.Tanh, scale=0.5
            )
            tanh_half[2 * b], tanh_half[2 * b + 1] = tanh_pair[:, 0, :], tanh_pair[:, 1, :]
            tanh_pairs[b] = tanh_pair

        def logarithms(pairs):
            for b in pairs:
                chain_pair = chain_pool.tile([P, 2, FEATURES], F32)
                nc.scalar.activation(
                    out=both(chain_pair),
                    in_=both(tanh_pairs[b]),
                    func=ACT.Ln,
                    scale=-0.5,
                    bias=halves[:, 0:1],
                )
                chain_pairs[b] = chain_pair
                chain[2 * b], chain[2 * b + 1] = chain_pair[:, 0, :], chain_pair[:, 1, :]
            for b in pairs:
                nc.scalar.activation(
                    out=both(chain_pairs[b]), in_=both(chain_pairs[b]), func=ACT.Ln, scale=-1.0
                )

        def inverse_cubes(part):
            nc.scalar.activation(out=part, in_=part, func=ACT.Exp, scale=-3.0)

        def product(bank, i, codes, scales, h):
            k, t = divmod(i, CHUNK_TILES)
            classes = slice(t * P, (t + 1) * P)
            for c in range(PASSES):
                nc.tensor.matmul_mx(
                    out=bank[:],
                    lhsT=e_codes[k][:, c, classes].bitcast(E5M2_X4),
                    lhsT_scale=e_scales[k][:, c, classes],
                    rhs=codes[:, c, piece(h)].bitcast(E4M3_X4),
                    rhs_scale=scales[:, c, piece(h)],
                    start=(c == 0),
                    stop=(c == PASSES - 1),
                )

        def first_moment(i):
            for h in range(FEATURE_HALVES):
                p1_bank = p1_pool.tile([P, WIDTH], F32)
                product(p1_bank, i, x_codes, x_scales, h)
                p1[i, h] = p1_bank

        def second_moment(i):
            for h in range(FEATURE_HALVES):
                p2_bank = p2_pool.tile([P, WIDTH], F32)
                product(p2_bank, i, xx_codes, xx_scales, h)
                p2[i, h] = p2_bank

        def mean_tile(i):
            k, t = divmod(i, CHUNK_TILES)
            return mean_rows[k][:, t, :]

        def mean_s0_minus_p1(i):
            k, t = divmod(i, CHUNK_TILES)
            q_tile = q_pool.tile([P, FEATURES], F32)
            for h in range(FEATURE_HALVES):
                nc.vector.scalar_tensor_tensor(
                    out=q_tile[:, piece(h)],
                    in0=mean_tile(i)[:, piece(h)],
                    scalar=half_s0[k][:, t, :],
                    in1=p1[i, h][:],
                    op0=ALU.mult,
                    op1=ALU.subtract,
                )
            q_tiles[i] = q_tile

        def times_mean(i):
            a_tile = a_pool.tile([P, FEATURES], F32)
            width = WIDTH if i == CLASS_TILES - 1 else FEATURES
            nc.gpsimd.tensor_tensor(
                out=a_tile[:, :width],
                in0=q_tiles[i][:, :width],
                in1=mean_tile(i)[:, :width],
                op=ALU.mult,
            )
            if width < FEATURES:
                nc.vector.tensor_tensor(
                    out=a_tile[:, width:],
                    in0=q_tiles[i][:, width:],
                    in1=mean_tile(i)[:, width:],
                    op=ALU.mult,
                )
            a_tiles[i] = a_tile

        def plus_half_p2(i):
            if i < FIRST_SPLIT_TILE:
                v_halves[i] = (a_tiles[i][:, piece(0)], a_tiles[i][:, piece(1)])
            else:
                b_tile = b_pool.tile([P, WIDTH], F32)
                v_halves[i] = (a_tiles[i][:, piece(0)], b_tile[:])
            for h in range(FEATURE_HALVES):
                nc.vector.scalar_tensor_tensor(
                    out=v_halves[i][h],
                    in0=p2[i, h][:],
                    scalar=0.5,
                    in1=a_tiles[i][:, piece(h)],
                    op0=ALU.mult,
                    op1=ALU.add,
                )

        def times_one_plus_tanh(i):
            y_tile = work_pool.tile([P, FEATURES], F32, tag="work", align_bytes=64)
            if i < FIRST_SPLIT_TILE:
                nc.vector.scalar_tensor_tensor(
                    out=y_tile[:],
                    in0=tanh_half[i],
                    scalar=1.0,
                    in1=a_tiles[i][:],
                    op0=ALU.add,
                    op1=ALU.mult,
                )
            else:
                for h in range(FEATURE_HALVES):
                    nc.vector.scalar_tensor_tensor(
                        out=y_tile[:, piece(h)],
                        in0=tanh_half[i][:, piece(h)],
                        scalar=1.0,
                        in1=v_halves[i][h],
                        op0=ALU.add,
                        op1=ALU.mult,
                    )
            y_tiles[i] = y_tile

        def finish(i):
            nc.vector.tensor_tensor(
                out=y_tiles[i][:], in0=y_tiles[i][:], in1=chain[i], op=ALU.mult
            )
            nc.sync.dma_start(out=out[i * P : (i + 1) * P, :], in_=y_tiles[i][:])

        first, second = slice(0, 2), slice(2, 4)
        for k in range(2):
            class_rows = rho_pool.tile([P, CHUNK_TILES, FEATURES], BF16)
            rho_rows[k] = class_rows
        class_rows = mean_pool.tile([P, CHUNK_TILES, FEATURES], BF16)
        mean_rows[0] = class_rows
        load_x_half(0, 0)
        load_x(1)
        load_quad(0, 0)
        load_grad(0, 0)
        load_quad(0, 1)
        load_x_half(0, 1)
        load_grad(0, 1)
        load_class_tiles(rho_rows[0], rho, 0, first)
        load_class_tiles(rho_rows[0], rho, 0, second)
        load_quad(1, 0)
        load_class_tiles(rho_rows[1], rho, 1, first)
        load_class_tiles(mean_rows[0], mean, 0, first)
        load_grad(1, 0)
        load_class_tiles(rho_rows[1], rho, 1, second)
        load_quad(1, 1)
        load_class_tiles(mean_rows[0], mean, 0, second)
        load_grad(1, 1)
        load_quad(2, 0)
        load_quad(2, 1)
        load_grad(2, 0)
        mean_rows[1] = load_class_rows(mean_pool, mean, 1)
        load_grad(2, 1)

        square_x_on_scalar(0, 0)
        regroup_x(0, 0)
        quantise_x(0, 0)
        regroup_x(1, 0)
        quantise_x(1, 0)
        quantise_square(0, 0)
        exponential(0, 0)
        regroup_x(1, 1)
        multiply(0, 0)
        sums_in_four_banks(0)
        for t in range(CHUNK_TILES):
            column_sums(0, t, (0,))
        square_x_on_scalar(1, 0)
        quantise_x(1, 1)
        quantise_square(1, 0)
        exponential(0, 1)
        regroup_x(0, 1)
        multiply(0, 1)
        for t in range(CHUNK_TILES):
            column_sums(0, t, (1,))
        regroup_e(0, 0)
        regroup_e(0, 1)
        quantise_x(0, 1)
        quantise_e(0)
        square_x(0, 1)
        square_x(1, 1)
        quantise_square(0, 1)
        quantise_square(1, 1)
        copy_sums(0)
        first_moment(0)
        copy_grad(1, 0, PACK)
        first_moment(1)
        tanh_rho(0)
        tanh_rho(1)
        exponential(1, 0)
        tanh_rho(2)
        tanh_rho(3)
        exponential(1, 1)

        last = CLASS_TILES - 1
        for s in range(-2, CLASS_TILES):
            if s >= 0:
                plus_half_p2(s)
            if s == -1:
                multiply_from_psum(1, 0, PACK)
                regroup_e(1, 0)
            if s + 2 <= last:
                mean_s0_minus_p1(s + 2)
            if 0 <= s + 1 <= last:
                times_mean(s + 1)

            following, phase = divmod(s + 6, CHUNK_TILES)
            make_e = 1 <= following < CHUNKS and s >= 0
            if make_e and phase == 1:
                multiply_from_psum(following, 1, VECTOR_ROWS)
            if make_e and phase == 2:
                if following == 1:
                    multiply_from_psum(1, 1, VECTOR_ROWS)

            late_results = 7 <= s <= 10
            if 0 <= s < FIRST_SPLIT_TILE and not late_results:
                times_one_plus_tanh(s)
            if make_e and phase == 0:
                multiply(following, 0)
                regroup_e(following, 0)
            if make_e and phase == 2:
                regroup_e(following, 1)
            if make_e and phase == 3:
                quantise_e(following)

            if s == -1:
                for c in range(PASSES):
                    exponential(2, c)
            if s in (-1, 2):
                logarithms((0, 1) if s < 0 else (2, 3))
            if s == 2:
                rho_rows[2] = load_class_rows(rho_pool, rho, 2)
                rho_rows[3] = load_class_rows(rho_pool, rho, 3)
            if s == 4:
                for c in range(PASSES):
                    load_quad(3, c)
                for c in range(PASSES):
                    load_grad(3, c)
                mean_rows[2] = load_class_rows(mean_pool, mean, 2)
                for c in range(PASSES):
                    exponential(3, c)
                inverse_cubes(both(chain_pairs[0]))
            if s == 5:
                inverse_cubes(both(chain_pairs[1]))
                tanh_rho(4)
            if s == 6:
                tanh_rho(5)
                inverse_cubes(both(chain_pairs[2]))
            if s == 7:
                inverse_cubes(both(chain_pairs[3]))
                tanh_rho(6)
                tanh_rho(7)
            if s == 8:
                mean_rows[3] = load_class_rows(mean_pool, mean, 3)
            if s in (8, 10):
                logarithms((4, 5) if s == 8 else (6, 7))
            if 12 <= s <= 15:
                inverse_cubes(chain[2 * s - 16])
                inverse_cubes(chain[2 * s - 15])

            if late_results:
                finish(2 * s - 14)
                times_one_plus_tanh(s)
                finish(2 * s - 13)
            if s >= FIRST_SPLIT_TILE:
                times_one_plus_tanh(s)

            if (s + 3) % CHUNK_TILES == 0 and 1 <= (s + 3) // CHUNK_TILES < CHUNKS:
                copy_sums_of_pair((s + 3) // CHUNK_TILES, 0)
            if (s + 1) % CHUNK_TILES == 0 and 1 <= (s + 1) // CHUNK_TILES < CHUNKS:
                copy_sums_of_pair((s + 1) // CHUNK_TILES, 1)

            if 0 <= s + 1 <= last:
                second_moment(s + 1)
            if 2 <= s + 3 <= last:
                first_moment(s + 3)
            if s in (-1, 2, 6):
                copy_grad((s + 6) // CHUNK_TILES, 1, VECTOR_ROWS)
            sums_chunk, sums_tile = divmod(s + 5, CHUNK_TILES)
            if s == 0:
                sums_in_one_bank(1)
                column_sums(1, 0)
            if 1 <= sums_chunk < CHUNKS and s >= 0:
                if sums_tile == 0:
                    sums_in_one_bank(sums_chunk)
                column_sums(sums_chunk, sums_tile)
        for i in range(ROUND_TILES, CLASS_TILES):
            finish(i)
